import numpy as np
import ml_dtypes

BF16 = ml_dtypes.bfloat16


def bf(x):
    return np.asarray(x, np.float32).astype(BF16)


def f32(x):
    return np.asarray(x, np.float32)


def f64(x):
    return np.asarray(x).astype(np.float64)


def striped(idx):
    return np.tile(idx.reshape(-1, 16).T, (8, 1))


C, S, K, H, E, N = 512, 2048, 3, 1024, 8, 3072


def setup_inputs():
    return {"x": f32(np.random.standard_normal((C, S))), "thr": f32(np.random.standard_normal((1, S))), "luts": f32(np.random.random((E, H))), "offs": striped(np.concatenate([np.random.permutation(S)[:H] for _ in range(K)]))}


def reference(x, thr, luts, offs):
    idx = offs[:16].T.reshape(-1)
    bits = np.where(f64(x) > f64(thr), 1.0, 0.0)
    u = bits[:, idx]
    acc = np.broadcast_to(f64(luts)[:, None, :], (E, C, H))
    for k in range(K):
        half = acc.shape[0] // 2
        uk = u[:, k * H:(k + 1) * H]
        acc = acc[:half] + uk[None, :, :] * (acc[half:] - acc[:half])
    return acc[0]

@@ -1,0 +1,59 @@
+import concourse.mybir as mybir
+
+F32 = mybir.dt.float32
+U16 = mybir.dt.uint16
+ALU = mybir.AluOpType
+
+P = 128
+C = 512
+S = 2048
+H = 1024
+PIECE = H // 16
+
+
+def tile_dwnmodel_kernel(tc, x, thr, luts, offs, out):
+    nc = tc.nc
+    with (
+        tc.tile_pool(name="held", bufs=1) as held,
+        tc.tile_pool(name="work", bufs=2) as work,
+    ):
+        offsets = held.tile([P, 3 * PIECE], U16, name="offsets")
+        nc.sync.dma_start(offsets[:], offs)
+
+        thr_all = held.tile([P, S], F32, name="thr_all")
+        nc.scalar.dma_start(thr_all[:], thr.rearrange("one s -> (one s)").partition_broadcast(P))
+        lut_all = held.tile([P, 8 * H], F32, name="lut_all")
+        nc.scalar.dma_start(lut_all[:], luts.rearrange("e o -> (e o)").partition_broadcast(P))
+
+        lut_diff = held.tile([P, 4 * H], F32, name="lut_diff")
+        nc.vector.tensor_sub(lut_diff[:], lut_all[:, 4 * H : 8 * H], lut_all[:, 0 : 4 * H])
+
+        for block in range(C // P):
+            x_block = work.tile([P, S], F32, name="x_block")
+            nc.sync.dma_start(x_block[:], x[block * P : (block + 1) * P, :])
+            bits = work.tile([P, S], F32, name="bits")
+            nc.vector.tensor_tensor(bits[:], x_block[:], thr_all[:], ALU.is_gt)
+
+            def picked(fold):
+                return bits[:].indirect(offsets[:, fold * PIECE : (fold + 1) * PIECE])
+
+            a = work.tile([P, 4 * H], F32, name="a")
+            for e in range(4):
+                entry = slice(e * H, (e + 1) * H)
+                nc.vector.tensor_tensor(a[:, entry], picked(0), lut_diff[:, entry], ALU.mult)
+            nc.vector.tensor_add(a[:], a[:], lut_all[:, 0 : 4 * H])
+
+            a_diff = work.tile([P, 2 * H], F32, name="a_diff")
+            nc.vector.tensor_sub(a_diff[:], a[:, 2 * H : 4 * H], a[:, 0 : 2 * H])
+            b = work.tile([P, 2 * H], F32, name="b")
+            for e in range(2):
+                entry = slice(e * H, (e + 1) * H)
+                nc.vector.tensor_tensor(b[:, entry], picked(1), a_diff[:, entry], ALU.mult)
+            nc.vector.tensor_add(b[:], b[:], a[:, 0 : 2 * H])
+
+            b_diff = work.tile([P, H], F32, name="b_diff")
+            nc.vector.tensor_sub(b_diff[:], b[:, H : 2 * H], b[:, 0:H])
+            result = work.tile([P, H], F32, name="result")
+            nc.vector.tensor_tensor(result[:], picked(2), b_diff[:], ALU.mult)
+            nc.vector.tensor_add(result[:], result[:], b[:, 0:H])
+            nc.sync.dma_start(out[block * P : (block + 1) * P, :], result[:])

@@ -1,4 +1,5 @@
 import concourse.mybir as mybir
+from concourse.masks import make_identity
 
 F32 = mybir.dt.float32
 U16 = mybir.dt.uint16
@@ -8,7 +9,15 @@ P = 128
 C = 512
 S = 2048
 H = 1024
+E = 8
 PIECE = H // 16
+BANK = 512
+
+LUT_DIFF = 0
+LUT_STEP = 4
+LUT_ONE_LESS_ZERO = 6
+LUT_ZERO = 7
+MIXES = 8
 
 
 def tile_dwnmodel_kernel(tc, x, thr, luts, offs, out):
@@ -20,40 +29,98 @@ def tile_dwnmodel_kernel(tc, x, thr, luts, offs, out):
         offsets = held.tile([P, 3 * PIECE], U16, name="offsets")
         nc.sync.dma_start(offsets[:], offs)
 
+        tables = held.tile([P, H], F32, name="tables")
+        nc.gpsimd.memset(tables[:], 0.0)
+        nc.sync.dma_start(tables[0:E, :], luts)
+
         thr_all = held.tile([P, S], F32, name="thr_all")
         nc.scalar.dma_start(thr_all[:], thr.rearrange("one s -> (one s)").partition_broadcast(P))
-        lut_all = held.tile([P, 8 * H], F32, name="lut_all")
-        nc.scalar.dma_start(lut_all[:], luts.rearrange("e o -> (e o)").partition_broadcast(P))
+
+        plus = held.tile([P, P], F32, name="plus")
+        make_identity(nc, plus[:])
+        minus = held.tile([P, P], F32, name="minus")
+        nc.vector.tensor_scalar_mul(minus[:], plus[:], -1.0)
+
+        mix = held.tile([P, MIXES], F32, name="mix")
+        nc.vector.tensor_sub(mix[:, LUT_DIFF : LUT_DIFF + 4], plus[:, 4:8], plus[:, 0:4])
+        nc.vector.tensor_sub(mix[:, LUT_STEP : LUT_STEP + 2], plus[:, 2:4], plus[:, 0:2])
+        nc.vector.tensor_sub(mix[:, LUT_ONE_LESS_ZERO : LUT_ONE_LESS_ZERO + 1], plus[:, 1:2], plus[:, 0:1])
+        nc.vector.tensor_copy(mix[:, LUT_ZERO : LUT_ZERO + 1], plus[:, 0:1])
+        spread = held.tile([P, MIXES, P], F32, name="spread")
+        nc.vector.tensor_copy(spread[:], mix[:].unsqueeze(2).to_broadcast([P, MIXES, P]))
+
+        def accumulate(total, weights, term, start=False, stop=False):
+            for bank in range(H // BANK):
+                cols = slice(bank * BANK, (bank + 1) * BANK)
+                nc.tensor.matmul(total[:, cols], weights, term[:, cols], start=start, stop=stop)
+
+        def copy_out(dest, total):
+            for bank in range(H // BANK):
+                cols = slice(bank * BANK, (bank + 1) * BANK)
+                nc.scalar.copy(dest[:, cols], total[:, cols])
 
         lut_diff = held.tile([P, 4 * H], F32, name="lut_diff")
-        nc.vector.tensor_sub(lut_diff[:], lut_all[:, 4 * H : 8 * H], lut_all[:, 0 : 4 * H])
+        lut_step = held.tile([P, 2 * H], F32, name="lut_step")
+        with tc.psum_pool(name="spread_sums", bufs=2) as spread_sums:
+            for dest, first_mix, count in ((lut_diff, LUT_DIFF, 4), (lut_step, LUT_STEP, 2)):
+                for e in range(count):
+                    spread_sum = spread_sums.tile([P, H], F32, name="spread_sum")
+                    accumulate(spread_sum, spread[:, first_mix + e, :], tables, start=True, stop=True)
+                    copy_out(dest[:, e * H : (e + 1) * H], spread_sum)
 
-        for block in range(C // P):
-            x_block = work.tile([P, S], F32, name="x_block")
-            nc.sync.dma_start(x_block[:], x[block * P : (block + 1) * P, :])
-            bits = work.tile([P, S], F32, name="bits")
-            nc.vector.tensor_tensor(bits[:], x_block[:], thr_all[:], ALU.is_gt)
-
-            def picked(fold):
+        with (
+            tc.psum_pool(name="diff_sums", bufs=2) as diff_sums,
+            tc.psum_pool(name="out_sums", bufs=2) as out_sums,
+        ):
+            def picked(bits, fold):
                 return bits[:].indirect(offsets[:, fold * PIECE : (fold + 1) * PIECE])
 
-            a = work.tile([P, 4 * H], F32, name="a")
-            for e in range(4):
-                entry = slice(e * H, (e + 1) * H)
-                nc.vector.tensor_tensor(a[:, entry], picked(0), lut_diff[:, entry], ALU.mult)
-            nc.vector.tensor_add(a[:], a[:], lut_all[:, 0 : 4 * H])
+            def folds_1_and_2(block):
+                x_block = work.tile([P, S], F32, name="x_block")
+                nc.sync.dma_start(x_block[:], x[block * P : (block + 1) * P, :])
+                bits = work.tile([P, S], F32, name="bits")
+                nc.vector.tensor_tensor(bits[:], x_block[:], thr_all[:], ALU.is_gt)
 
-            a_diff = work.tile([P, 2 * H], F32, name="a_diff")
-            nc.vector.tensor_sub(a_diff[:], a[:, 2 * H : 4 * H], a[:, 0 : 2 * H])
-            b = work.tile([P, 2 * H], F32, name="b")
-            for e in range(2):
-                entry = slice(e * H, (e + 1) * H)
-                nc.vector.tensor_tensor(b[:, entry], picked(1), a_diff[:, entry], ALU.mult)
-            nc.vector.tensor_add(b[:], b[:], a[:, 0 : 2 * H])
+                p = work.tile([P, 4 * H], F32, name="p")
+                for e in range(4):
+                    entry = slice(e * H, (e + 1) * H)
+                    nc.vector.tensor_tensor(p[:, entry], picked(bits, 0), lut_diff[:, entry], ALU.mult)
 
-            b_diff = work.tile([P, H], F32, name="b_diff")
-            nc.vector.tensor_sub(b_diff[:], b[:, H : 2 * H], b[:, 0:H])
-            result = work.tile([P, H], F32, name="result")
-            nc.vector.tensor_tensor(result[:], picked(2), b_diff[:], ALU.mult)
-            nc.vector.tensor_add(result[:], result[:], b[:, 0:H])
-            nc.sync.dma_start(out[block * P : (block + 1) * P, :], result[:])
+                b_diff_sum = diff_sums.tile([P, H], F32, name="b_diff_sum")
+                accumulate(b_diff_sum, spread[:, LUT_ONE_LESS_ZERO, :], tables, start=True)
+                accumulate(b_diff_sum, minus[:], p[:, 0:H])
+                accumulate(b_diff_sum, plus[:], p[:, H : 2 * H])
+                out_sum = out_sums.tile([P, H], F32, name="out_sum")
+                accumulate(out_sum, spread[:, LUT_ZERO, :], tables, start=True)
+                accumulate(out_sum, plus[:], p[:, 0:H])
+
+                a_diff = work.tile([P, 2 * H], F32, name="a_diff")
+                nc.vector.tensor_sub(a_diff[:], p[:, 2 * H : 4 * H], p[:, 0 : 2 * H])
+                nc.vector.tensor_add(a_diff[:], a_diff[:], lut_step[:])
+                q = work.tile([P, 2 * H], F32, name="q")
+                for e in range(2):
+                    entry = slice(e * H, (e + 1) * H)
+                    nc.vector.tensor_tensor(q[:, entry], picked(bits, 1), a_diff[:, entry], ALU.mult)
+
+                accumulate(b_diff_sum, minus[:], q[:, 0:H])
+                accumulate(b_diff_sum, plus[:], q[:, H : 2 * H], stop=True)
+                accumulate(out_sum, plus[:], q[:, 0:H])
+                b_diff = work.tile([P, H], F32, name="b_diff")
+                copy_out(b_diff, b_diff_sum)
+                return bits, b_diff, out_sum
+
+            def fold_3(block, bits, b_diff, out_sum):
+                s = work.tile([P, H], F32, name="s")
+                nc.vector.tensor_tensor(s[:], picked(bits, 2), b_diff[:], ALU.mult)
+                accumulate(out_sum, plus[:], s, stop=True)
+                result = work.tile([P, H], F32, name="result")
+                copy_out(result, out_sum)
+                nc.scalar.dma_start(out[block * P : (block + 1) * P, :], result[:])
+
+            blocks = C // P
+            waiting = folds_1_and_2(0)
+            for block in range(1, blocks):
+                following = folds_1_and_2(block)
+                fold_3(block - 1, *waiting)
+                waiting = following
+            fold_3(blocks - 1, *waiting)

@@ -25,6 +25,7 @@ def tile_dwnmodel_kernel(tc, x, thr, luts, offs, out):
     with (
         tc.tile_pool(name="held", bufs=1) as held,
         tc.tile_pool(name="work", bufs=2) as work,
+        tc.tile_pool(name="long", bufs=3) as long_lived,
     ):
         offsets = held.tile([P, 3 * PIECE], U16, name="offsets")
         nc.sync.dma_start(offsets[:], offs)
@@ -39,15 +40,15 @@ def tile_dwnmodel_kernel(tc, x, thr, luts, offs, out):
         plus = held.tile([P, P], F32, name="plus")
         make_identity(nc, plus[:])
         minus = held.tile([P, P], F32, name="minus")
-        nc.vector.tensor_scalar_mul(minus[:], plus[:], -1.0)
+        nc.gpsimd.tensor_scalar_mul(minus[:], plus[:], -1.0)
 
         mix = held.tile([P, MIXES], F32, name="mix")
-        nc.vector.tensor_sub(mix[:, LUT_DIFF : LUT_DIFF + 4], plus[:, 4:8], plus[:, 0:4])
-        nc.vector.tensor_sub(mix[:, LUT_STEP : LUT_STEP + 2], plus[:, 2:4], plus[:, 0:2])
-        nc.vector.tensor_sub(mix[:, LUT_ONE_LESS_ZERO : LUT_ONE_LESS_ZERO + 1], plus[:, 1:2], plus[:, 0:1])
-        nc.vector.tensor_copy(mix[:, LUT_ZERO : LUT_ZERO + 1], plus[:, 0:1])
+        nc.gpsimd.tensor_sub(mix[:, LUT_DIFF : LUT_DIFF + 4], plus[:, 4:8], plus[:, 0:4])
+        nc.gpsimd.tensor_sub(mix[:, LUT_STEP : LUT_STEP + 2], plus[:, 2:4], plus[:, 0:2])
+        nc.gpsimd.tensor_sub(mix[:, LUT_ONE_LESS_ZERO : LUT_ONE_LESS_ZERO + 1], plus[:, 1:2], plus[:, 0:1])
+        nc.gpsimd.tensor_copy(mix[:, LUT_ZERO : LUT_ZERO + 1], plus[:, 0:1])
         spread = held.tile([P, MIXES, P], F32, name="spread")
-        nc.vector.tensor_copy(spread[:], mix[:].unsqueeze(2).to_broadcast([P, MIXES, P]))
+        nc.gpsimd.tensor_copy(spread[:], mix[:].unsqueeze(2).to_broadcast([P, MIXES, P]))
 
         def accumulate(total, weights, term, start=False, stop=False):
             for bank in range(H // BANK):
@@ -78,10 +79,10 @@ def tile_dwnmodel_kernel(tc, x, thr, luts, offs, out):
             def folds_1_and_2(block):
                 x_block = work.tile([P, S], F32, name="x_block")
                 nc.sync.dma_start(x_block[:], x[block * P : (block + 1) * P, :])
-                bits = work.tile([P, S], F32, name="bits")
+                bits = long_lived.tile([P, S], F32, name="bits")
                 nc.vector.tensor_tensor(bits[:], x_block[:], thr_all[:], ALU.is_gt)
 
-                p = work.tile([P, 4 * H], F32, name="p")
+                p = long_lived.tile([P, 4 * H], F32, name="p")
                 for e in range(4):
                     entry = slice(e * H, (e + 1) * H)
                     nc.vector.tensor_tensor(p[:, entry], picked(bits, 0), lut_diff[:, entry], ALU.mult)
@@ -95,8 +96,10 @@ def tile_dwnmodel_kernel(tc, x, thr, luts, offs, out):
                 accumulate(out_sum, plus[:], p[:, 0:H])
 
                 a_diff = work.tile([P, 2 * H], F32, name="a_diff")
-                nc.vector.tensor_sub(a_diff[:], p[:, 2 * H : 4 * H], p[:, 0 : 2 * H])
-                nc.vector.tensor_add(a_diff[:], a_diff[:], lut_step[:])
+                for e in range(2):
+                    entry = slice(e * H, (e + 1) * H)
+                    nc.gpsimd.tensor_sub(a_diff[:, entry], p[:, (2 + e) * H : (3 + e) * H], p[:, entry])
+                    nc.gpsimd.tensor_add(a_diff[:, entry], a_diff[:, entry], lut_step[:, entry])
                 q = work.tile([P, 2 * H], F32, name="q")
                 for e in range(2):
                     entry = slice(e * H, (e + 1) * H)

@@ -13,11 +13,10 @@ E = 8
 PIECE = H // 16
 BANK = 512
 
-LUT_DIFF = 0
-LUT_STEP = 4
-LUT_ONE_LESS_ZERO = 6
-LUT_ZERO = 7
-MIXES = 8
+LOW = 0
+HIGH = 4
+STEP = 8
+MIXES = 12
 
 
 def tile_dwnmodel_kernel(tc, x, thr, luts, offs, out):
@@ -25,7 +24,6 @@ def tile_dwnmodel_kernel(tc, x, thr, luts, offs, out):
     with (
         tc.tile_pool(name="held", bufs=1) as held,
         tc.tile_pool(name="work", bufs=2) as work,
-        tc.tile_pool(name="long", bufs=3) as long_lived,
     ):
         offsets = held.tile([P, 3 * PIECE], U16, name="offsets")
         nc.sync.dma_start(offsets[:], offs)
@@ -39,16 +37,22 @@ def tile_dwnmodel_kernel(tc, x, thr, luts, offs, out):
 
         plus = held.tile([P, P], F32, name="plus")
         make_identity(nc, plus[:])
-        minus = held.tile([P, P], F32, name="minus")
-        nc.gpsimd.tensor_scalar_mul(minus[:], plus[:], -1.0)
 
         mix = held.tile([P, MIXES], F32, name="mix")
-        nc.gpsimd.tensor_sub(mix[:, LUT_DIFF : LUT_DIFF + 4], plus[:, 4:8], plus[:, 0:4])
-        nc.gpsimd.tensor_sub(mix[:, LUT_STEP : LUT_STEP + 2], plus[:, 2:4], plus[:, 0:2])
-        nc.gpsimd.tensor_sub(mix[:, LUT_ONE_LESS_ZERO : LUT_ONE_LESS_ZERO + 1], plus[:, 1:2], plus[:, 0:1])
-        nc.gpsimd.tensor_copy(mix[:, LUT_ZERO : LUT_ZERO + 1], plus[:, 0:1])
+        rows = plus[:, 0:E].rearrange("k (half e) -> k half e", half=2)
+        low_high = mix[:, LOW : LOW + E].rearrange("k (half j) -> k half j", half=2)
+        nc.gpsimd.tensor_copy(low_high[:, :, 0:1], rows[:, :, 0:1])
+        nc.gpsimd.tensor_sub(low_high[:, :, 1:2], rows[:, :, 1:2], rows[:, :, 0:1])
+        nc.gpsimd.tensor_sub(low_high[:, :, 2:4], rows[:, :, 2:4], rows[:, :, 0:2])
+        nc.gpsimd.tensor_sub(mix[:, STEP : STEP + 4], mix[:, HIGH : HIGH + 4], mix[:, LOW : LOW + 4])
         spread = held.tile([P, MIXES, P], F32, name="spread")
-        nc.gpsimd.tensor_copy(spread[:], mix[:].unsqueeze(2).to_broadcast([P, MIXES, P]))
+        for group in (STEP, LOW):
+            nc.gpsimd.tensor_copy(
+                spread[:, group : group + 4, :],
+                mix[:, group : group + 4].unsqueeze(2).to_broadcast([P, 4, P]),
+            )
+        minus = held.tile([P, P], F32, name="minus")
+        nc.gpsimd.tensor_scalar_mul(minus[:], plus[:], -1.0)
 
         def accumulate(total, weights, term, start=False, stop=False):
             for bank in range(H // BANK):
@@ -60,50 +64,47 @@ def tile_dwnmodel_kernel(tc, x, thr, luts, offs, out):
                 cols = slice(bank * BANK, (bank + 1) * BANK)
                 nc.scalar.copy(dest[:, cols], total[:, cols])
 
-        lut_diff = held.tile([P, 4 * H], F32, name="lut_diff")
-        lut_step = held.tile([P, 2 * H], F32, name="lut_step")
+        step_all = held.tile([P, 4 * H], F32, name="step_all")
+        low_23 = held.tile([P, 2 * H], F32, name="low_23")
         with tc.psum_pool(name="spread_sums", bufs=2) as spread_sums:
-            for dest, first_mix, count in ((lut_diff, LUT_DIFF, 4), (lut_step, LUT_STEP, 2)):
-                for e in range(count):
+            for dest, first_mix, count in ((step_all, STEP, 4), (low_23, LOW + 2, 2)):
+                for j in range(count):
                     spread_sum = spread_sums.tile([P, H], F32, name="spread_sum")
-                    accumulate(spread_sum, spread[:, first_mix + e, :], tables, start=True, stop=True)
-                    copy_out(dest[:, e * H : (e + 1) * H], spread_sum)
+                    accumulate(spread_sum, spread[:, first_mix + j, :], tables, start=True, stop=True)
+                    copy_out(dest[:, j * H : (j + 1) * H], spread_sum)
 
         with (
             tc.psum_pool(name="diff_sums", bufs=2) as diff_sums,
             tc.psum_pool(name="out_sums", bufs=2) as out_sums,
         ):
+
             def picked(bits, fold):
                 return bits[:].indirect(offsets[:, fold * PIECE : (fold + 1) * PIECE])
 
             def folds_1_and_2(block):
                 x_block = work.tile([P, S], F32, name="x_block")
                 nc.sync.dma_start(x_block[:], x[block * P : (block + 1) * P, :])
-                bits = long_lived.tile([P, S], F32, name="bits")
+                bits = work.tile([P, S], F32, name="bits")
                 nc.vector.tensor_tensor(bits[:], x_block[:], thr_all[:], ALU.is_gt)
 
-                p = long_lived.tile([P, 4 * H], F32, name="p")
-                for e in range(4):
-                    entry = slice(e * H, (e + 1) * H)
-                    nc.vector.tensor_tensor(p[:, entry], picked(bits, 0), lut_diff[:, entry], ALU.mult)
+                p = work.tile([P, 4 * H], F32, name="p")
+                for j in range(4):
+                    part = slice(j * H, (j + 1) * H)
+                    nc.vector.tensor_tensor(p[:, part], picked(bits, 0), step_all[:, part], ALU.mult)
 
                 b_diff_sum = diff_sums.tile([P, H], F32, name="b_diff_sum")
-                accumulate(b_diff_sum, spread[:, LUT_ONE_LESS_ZERO, :], tables, start=True)
-                accumulate(b_diff_sum, minus[:], p[:, 0:H])
+                accumulate(b_diff_sum, spread[:, LOW + 1, :], tables, start=True)
                 accumulate(b_diff_sum, plus[:], p[:, H : 2 * H])
                 out_sum = out_sums.tile([P, H], F32, name="out_sum")
-                accumulate(out_sum, spread[:, LUT_ZERO, :], tables, start=True)
+                accumulate(out_sum, spread[:, LOW, :], tables, start=True)
                 accumulate(out_sum, plus[:], p[:, 0:H])
 
                 a_diff = work.tile([P, 2 * H], F32, name="a_diff")
-                for e in range(2):
-                    entry = slice(e * H, (e + 1) * H)
-                    nc.gpsimd.tensor_sub(a_diff[:, entry], p[:, (2 + e) * H : (3 + e) * H], p[:, entry])
-                    nc.gpsimd.tensor_add(a_diff[:, entry], a_diff[:, entry], lut_step[:, entry])
+                nc.vector.tensor_add(a_diff[:], p[:, 2 * H : 4 * H], low_23[:])
                 q = work.tile([P, 2 * H], F32, name="q")
                 for e in range(2):
-                    entry = slice(e * H, (e + 1) * H)
-                    nc.vector.tensor_tensor(q[:, entry], picked(bits, 1), a_diff[:, entry], ALU.mult)
+                    part = slice(e * H, (e + 1) * H)
+                    nc.vector.tensor_tensor(q[:, part], picked(bits, 1), a_diff[:, part], ALU.mult)
 
                 accumulate(b_diff_sum, minus[:], q[:, 0:H])
                 accumulate(b_diff_sum, plus[:], q[:, H : 2 * H], stop=True)

@@ -12,6 +12,7 @@ H = 1024
 E = 8
 PIECE = H // 16
 BANK = 512
+BANKS = H // BANK
 
 LOW = 0
 HIGH = 4
@@ -54,15 +55,14 @@ def tile_dwnmodel_kernel(tc, x, thr, luts, offs, out):
         minus = held.tile([P, P], F32, name="minus")
         nc.gpsimd.tensor_scalar_mul(minus[:], plus[:], -1.0)
 
-        def accumulate(total, weights, term, start=False, stop=False):
-            for bank in range(H // BANK):
-                cols = slice(bank * BANK, (bank + 1) * BANK)
-                nc.tensor.matmul(total[:, cols], weights, term[:, cols], start=start, stop=stop)
+        def bank_of(tile_or_view, bank):
+            return tile_or_view[:, bank * BANK : (bank + 1) * BANK]
 
-        def copy_out(dest, total):
-            for bank in range(H // BANK):
-                cols = slice(bank * BANK, (bank + 1) * BANK)
-                nc.scalar.copy(dest[:, cols], total[:, cols])
+        def accumulate(total, weights, term, bank, start=False, stop=False):
+            nc.tensor.matmul(bank_of(total, bank), weights, bank_of(term, bank), start=start, stop=stop)
+
+        def copy_out(dest, total, bank):
+            nc.scalar.copy(bank_of(dest, bank), bank_of(total, bank))
 
         step_all = held.tile([P, 4 * H], F32, name="step_all")
         low_23 = held.tile([P, 2 * H], F32, name="low_23")
@@ -70,16 +70,17 @@ def tile_dwnmodel_kernel(tc, x, thr, luts, offs, out):
             for dest, first_mix, count in ((step_all, STEP, 4), (low_23, LOW + 2, 2)):
                 for j in range(count):
                     spread_sum = spread_sums.tile([P, H], F32, name="spread_sum")
-                    accumulate(spread_sum, spread[:, first_mix + j, :], tables, start=True, stop=True)
-                    copy_out(dest[:, j * H : (j + 1) * H], spread_sum)
+                    for bank in range(BANKS):
+                        accumulate(spread_sum, spread[:, first_mix + j, :], tables, bank, start=True, stop=True)
+                        copy_out(dest[:, j * H : (j + 1) * H], spread_sum, bank)
 
         with (
             tc.psum_pool(name="diff_sums", bufs=2) as diff_sums,
             tc.psum_pool(name="out_sums", bufs=2) as out_sums,
         ):
 
-            def picked(bits, fold):
-                return bits[:].indirect(offsets[:, fold * PIECE : (fold + 1) * PIECE])
+            def picked(bits, first, count):
+                return bits[:].indirect(offsets[:, first // 16 : (first + count) // 16])
 
             def folds_1_and_2(block):
                 x_block = work.tile([P, S], F32, name="x_block")
@@ -90,36 +91,47 @@ def tile_dwnmodel_kernel(tc, x, thr, luts, offs, out):
                 p = work.tile([P, 4 * H], F32, name="p")
                 for j in range(4):
                     part = slice(j * H, (j + 1) * H)
-                    nc.vector.tensor_tensor(p[:, part], picked(bits, 0), step_all[:, part], ALU.mult)
+                    nc.vector.tensor_tensor(p[:, part], picked(bits, 0, H), step_all[:, part], ALU.mult)
 
                 b_diff_sum = diff_sums.tile([P, H], F32, name="b_diff_sum")
-                accumulate(b_diff_sum, spread[:, LOW + 1, :], tables, start=True)
-                accumulate(b_diff_sum, plus[:], p[:, H : 2 * H])
                 out_sum = out_sums.tile([P, H], F32, name="out_sum")
-                accumulate(out_sum, spread[:, LOW, :], tables, start=True)
-                accumulate(out_sum, plus[:], p[:, 0:H])
+                for bank in range(BANKS):
+                    accumulate(b_diff_sum, spread[:, LOW + 1, :], tables, bank, start=True)
+                    accumulate(b_diff_sum, plus[:], p[:, H : 2 * H], bank)
+                for bank in range(BANKS):
+                    accumulate(out_sum, spread[:, LOW, :], tables, bank, start=True)
+                    accumulate(out_sum, plus[:], p[:, 0:H], bank)
 
                 a_diff = work.tile([P, 2 * H], F32, name="a_diff")
                 nc.vector.tensor_add(a_diff[:], p[:, 2 * H : 4 * H], low_23[:])
-                q = work.tile([P, 2 * H], F32, name="q")
-                for e in range(2):
-                    part = slice(e * H, (e + 1) * H)
-                    nc.vector.tensor_tensor(q[:, part], picked(bits, 1), a_diff[:, part], ALU.mult)
 
-                accumulate(b_diff_sum, minus[:], q[:, 0:H])
-                accumulate(b_diff_sum, plus[:], q[:, H : 2 * H], stop=True)
-                accumulate(out_sum, plus[:], q[:, 0:H])
+                q = work.tile([P, 2 * H], F32, name="q")
                 b_diff = work.tile([P, H], F32, name="b_diff")
-                copy_out(b_diff, b_diff_sum)
+                for bank in range(BANKS):
+                    for e in range(2):
+                        part = slice(e * H, (e + 1) * H)
+                        nc.vector.tensor_tensor(
+                            bank_of(q[:, part], bank),
+                            picked(bits, H + bank * BANK, BANK),
+                            bank_of(a_diff[:, part], bank),
+                            ALU.mult,
+                        )
+                    accumulate(b_diff_sum, minus[:], q[:, 0:H], bank)
+                    accumulate(b_diff_sum, plus[:], q[:, H : 2 * H], bank, stop=True)
+                    copy_out(b_diff, b_diff_sum, bank)
+                    accumulate(out_sum, plus[:], q[:, 0:H], bank)
                 return bits, b_diff, out_sum
 
             def fold_3(block, bits, b_diff, out_sum):
                 s = work.tile([P, H], F32, name="s")
-                nc.vector.tensor_tensor(s[:], picked(bits, 2), b_diff[:], ALU.mult)
-                accumulate(out_sum, plus[:], s, stop=True)
                 result = work.tile([P, H], F32, name="result")
-                copy_out(result, out_sum)
-                nc.scalar.dma_start(out[block * P : (block + 1) * P, :], result[:])
+                for bank in range(BANKS):
+                    nc.vector.tensor_tensor(
+                        bank_of(s, bank), picked(bits, 2 * H + bank * BANK, BANK), bank_of(b_diff, bank), ALU.mult
+                    )
+                    accumulate(out_sum, plus[:], s, bank, stop=True)
+                    copy_out(result, out_sum, bank)
+                    nc.scalar.dma_start(bank_of(out[block * P : (block + 1) * P, :], bank), bank_of(result, bank))
 
             blocks = C // P
             waiting = folds_1_and_2(0)

@@ -8,11 +8,11 @@ ALU = mybir.AluOpType
 P = 128
 C = 512
 S = 2048
+HALF = S // 2
 H = 1024
 E = 8
 PIECE = H // 16
 BANK = 512
-BANKS = H // BANK
 
 LOW = 0
 HIGH = 4
@@ -30,11 +30,16 @@ def tile_dwnmodel_kernel(tc, x, thr, luts, offs, out):
         nc.sync.dma_start(offsets[:], offs)
 
         tables = held.tile([P, H], F32, name="tables")
-        nc.gpsimd.memset(tables[:], 0.0)
-        nc.sync.dma_start(tables[0:E, :], luts)
+        for first in range(0, 32, E):
+            nc.sync.dma_start(tables[first : first + E, :], luts)
+        nc.vector.memset(tables[32:64, :], 0.0)
+        nc.vector.memset(tables[64:128, :], 0.0)
 
         thr_all = held.tile([P, S], F32, name="thr_all")
-        nc.scalar.dma_start(thr_all[:], thr.rearrange("one s -> (one s)").partition_broadcast(P))
+        thr_row = thr.rearrange("one s -> (one s)")
+        for half in range(2):
+            cols = slice(half * HALF, (half + 1) * HALF)
+            nc.scalar.dma_start(thr_all[:, cols], thr_row[cols].partition_broadcast(P))
 
         plus = held.tile([P, P], F32, name="plus")
         make_identity(nc, plus[:])
@@ -55,14 +60,15 @@ def tile_dwnmodel_kernel(tc, x, thr, luts, offs, out):
         minus = held.tile([P, P], F32, name="minus")
         nc.gpsimd.tensor_scalar_mul(minus[:], plus[:], -1.0)
 
-        def bank_of(tile_or_view, bank):
-            return tile_or_view[:, bank * BANK : (bank + 1) * BANK]
+        def accumulate(total, weights, term, start=False, stop=False):
+            for bank in range(H // BANK):
+                cols = slice(bank * BANK, (bank + 1) * BANK)
+                nc.tensor.matmul(total[:, cols], weights, term[:, cols], start=start, stop=stop)
 
-        def accumulate(total, weights, term, bank, start=False, stop=False):
-            nc.tensor.matmul(bank_of(total, bank), weights, bank_of(term, bank), start=start, stop=stop)
-
-        def copy_out(dest, total, bank):
-            nc.scalar.copy(bank_of(dest, bank), bank_of(total, bank))
+        def copy_out(dest, total):
+            for bank in range(H // BANK):
+                cols = slice(bank * BANK, (bank + 1) * BANK)
+                nc.scalar.copy(dest[:, cols], total[:, cols])
 
         step_all = held.tile([P, 4 * H], F32, name="step_all")
         low_23 = held.tile([P, 2 * H], F32, name="low_23")
@@ -70,68 +76,58 @@ def tile_dwnmodel_kernel(tc, x, thr, luts, offs, out):
             for dest, first_mix, count in ((step_all, STEP, 4), (low_23, LOW + 2, 2)):
                 for j in range(count):
                     spread_sum = spread_sums.tile([P, H], F32, name="spread_sum")
-                    for bank in range(BANKS):
-                        accumulate(spread_sum, spread[:, first_mix + j, :], tables, bank, start=True, stop=True)
-                        copy_out(dest[:, j * H : (j + 1) * H], spread_sum, bank)
+                    accumulate(spread_sum, spread[:, first_mix + j, :], tables, start=True, stop=True)
+                    copy_out(dest[:, j * H : (j + 1) * H], spread_sum)
 
         with (
             tc.psum_pool(name="diff_sums", bufs=2) as diff_sums,
             tc.psum_pool(name="out_sums", bufs=2) as out_sums,
         ):
 
-            def picked(bits, first, count):
-                return bits[:].indirect(offsets[:, first // 16 : (first + count) // 16])
+            def picked(bits, fold):
+                return bits[:].indirect(offsets[:, fold * PIECE : (fold + 1) * PIECE])
 
             def folds_1_and_2(block):
                 x_block = work.tile([P, S], F32, name="x_block")
-                nc.sync.dma_start(x_block[:], x[block * P : (block + 1) * P, :])
                 bits = work.tile([P, S], F32, name="bits")
-                nc.vector.tensor_tensor(bits[:], x_block[:], thr_all[:], ALU.is_gt)
+                for half in range(2):
+                    cols = slice(half * HALF, (half + 1) * HALF)
+                    nc.sync.dma_start(x_block[:, cols], x[block * P : (block + 1) * P, cols])
+                    nc.vector.tensor_tensor(bits[:, cols], x_block[:, cols], thr_all[:, cols], ALU.is_gt)
 
                 p = work.tile([P, 4 * H], F32, name="p")
                 for j in range(4):
                     part = slice(j * H, (j + 1) * H)
-                    nc.vector.tensor_tensor(p[:, part], picked(bits, 0, H), step_all[:, part], ALU.mult)
+                    nc.vector.tensor_tensor(p[:, part], picked(bits, 0), step_all[:, part], ALU.mult)
 
                 b_diff_sum = diff_sums.tile([P, H], F32, name="b_diff_sum")
+                accumulate(b_diff_sum, spread[:, LOW + 1, :], tables, start=True)
+                accumulate(b_diff_sum, plus[:], p[:, H : 2 * H])
                 out_sum = out_sums.tile([P, H], F32, name="out_sum")
-                for bank in range(BANKS):
-                    accumulate(b_diff_sum, spread[:, LOW + 1, :], tables, bank, start=True)
-                    accumulate(b_diff_sum, plus[:], p[:, H : 2 * H], bank)
-                for bank in range(BANKS):
-                    accumulate(out_sum, spread[:, LOW, :], tables, bank, start=True)
-                    accumulate(out_sum, plus[:], p[:, 0:H], bank)
+                accumulate(out_sum, spread[:, LOW, :], tables, start=True)
+                accumulate(out_sum, plus[:], p[:, 0:H])
 
                 a_diff = work.tile([P, 2 * H], F32, name="a_diff")
                 nc.vector.tensor_add(a_diff[:], p[:, 2 * H : 4 * H], low_23[:])
-
                 q = work.tile([P, 2 * H], F32, name="q")
+                for e in (1, 0):
+                    part = slice(e * H, (e + 1) * H)
+                    nc.vector.tensor_tensor(q[:, part], picked(bits, 1), a_diff[:, part], ALU.mult)
+
+                accumulate(b_diff_sum, plus[:], q[:, H : 2 * H])
+                accumulate(b_diff_sum, minus[:], q[:, 0:H], stop=True)
+                accumulate(out_sum, plus[:], q[:, 0:H])
                 b_diff = work.tile([P, H], F32, name="b_diff")
-                for bank in range(BANKS):
-                    for e in range(2):
-                        part = slice(e * H, (e + 1) * H)
-                        nc.vector.tensor_tensor(
-                            bank_of(q[:, part], bank),
-                            picked(bits, H + bank * BANK, BANK),
-                            bank_of(a_diff[:, part], bank),
-                            ALU.mult,
-                        )
-                    accumulate(b_diff_sum, minus[:], q[:, 0:H], bank)
-                    accumulate(b_diff_sum, plus[:], q[:, H : 2 * H], bank, stop=True)
-                    copy_out(b_diff, b_diff_sum, bank)
-                    accumulate(out_sum, plus[:], q[:, 0:H], bank)
+                copy_out(b_diff, b_diff_sum)
                 return bits, b_diff, out_sum
 
             def fold_3(block, bits, b_diff, out_sum):
                 s = work.tile([P, H], F32, name="s")
+                nc.vector.tensor_tensor(s[:], picked(bits, 2), b_diff[:], ALU.mult)
+                accumulate(out_sum, plus[:], s, stop=True)
                 result = work.tile([P, H], F32, name="result")
-                for bank in range(BANKS):
-                    nc.vector.tensor_tensor(
-                        bank_of(s, bank), picked(bits, 2 * H + bank * BANK, BANK), bank_of(b_diff, bank), ALU.mult
-                    )
-                    accumulate(out_sum, plus[:], s, bank, stop=True)
-                    copy_out(result, out_sum, bank)
-                    nc.scalar.dma_start(bank_of(out[block * P : (block + 1) * P, :], bank), bank_of(result, bank))
+                copy_out(result, out_sum)
+                nc.scalar.dma_start(out[block * P : (block + 1) * P, :], result[:])
 
             blocks = C // P
             waiting = folds_1_and_2(0)

@@ -24,16 +24,17 @@ def tile_dwnmodel_kernel(tc, x, thr, luts, offs, out):
     nc = tc.nc
     with (
         tc.tile_pool(name="held", bufs=1) as held,
-        tc.tile_pool(name="work", bufs=2) as work,
+        tc.tile_pool(name="loaded", bufs=1) as loaded,
+        tc.tile_pool(name="work", bufs=3) as work,
     ):
-        offsets = held.tile([P, 3 * PIECE], U16, name="offsets")
-        nc.sync.dma_start(offsets[:], offs)
-
         tables = held.tile([P, H], F32, name="tables")
-        for first in range(0, 32, E):
-            nc.sync.dma_start(tables[first : first + E, :], luts)
+        for first, queue in ((0, nc.sync), (E, nc.scalar), (2 * E, nc.sync), (3 * E, nc.scalar)):
+            queue.dma_start(tables[first : first + E, :], luts)
         nc.vector.memset(tables[32:64, :], 0.0)
         nc.vector.memset(tables[64:128, :], 0.0)
+
+        offsets = held.tile([P, 3 * PIECE], U16, name="offsets")
+        nc.sync.dma_start(offsets[:], offs)
 
         thr_all = held.tile([P, S], F32, name="thr_all")
         thr_row = thr.rearrange("one s -> (one s)")
@@ -45,11 +46,11 @@ def tile_dwnmodel_kernel(tc, x, thr, luts, offs, out):
         make_identity(nc, plus[:])
 
         mix = held.tile([P, MIXES], F32, name="mix")
-        rows = plus[:, 0:E].rearrange("k (half e) -> k half e", half=2)
-        low_high = mix[:, LOW : LOW + E].rearrange("k (half j) -> k half j", half=2)
-        nc.gpsimd.tensor_copy(low_high[:, :, 0:1], rows[:, :, 0:1])
-        nc.gpsimd.tensor_sub(low_high[:, :, 1:2], rows[:, :, 1:2], rows[:, :, 0:1])
-        nc.gpsimd.tensor_sub(low_high[:, :, 2:4], rows[:, :, 2:4], rows[:, :, 0:2])
+        nc.gpsimd.tensor_copy(mix[:, 0:E], plus[:, 0:E])
+        ones = mix[:, 0:E].rearrange("k (rest one) -> k rest one", one=2)
+        nc.gpsimd.tensor_sub(ones[:, :, 1:2], ones[:, :, 1:2], ones[:, :, 0:1])
+        twos = mix[:, 0:E].rearrange("k (rest two one) -> k rest two one", two=2, one=2)
+        nc.gpsimd.tensor_sub(twos[:, :, 1:2, :], twos[:, :, 1:2, :], twos[:, :, 0:1, :])
         nc.gpsimd.tensor_sub(mix[:, STEP : STEP + 4], mix[:, HIGH : HIGH + 4], mix[:, LOW : LOW + 4])
         spread = held.tile([P, MIXES, P], F32, name="spread")
         for group in (STEP, LOW):
@@ -57,8 +58,6 @@ def tile_dwnmodel_kernel(tc, x, thr, luts, offs, out):
                 spread[:, group : group + 4, :],
                 mix[:, group : group + 4].unsqueeze(2).to_broadcast([P, 4, P]),
             )
-        minus = held.tile([P, P], F32, name="minus")
-        nc.gpsimd.tensor_scalar_mul(minus[:], plus[:], -1.0)
 
         def accumulate(total, weights, term, start=False, stop=False):
             for bank in range(H // BANK):
@@ -73,8 +72,8 @@ def tile_dwnmodel_kernel(tc, x, thr, luts, offs, out):
         step_all = held.tile([P, 4 * H], F32, name="step_all")
         low_23 = held.tile([P, 2 * H], F32, name="low_23")
         with tc.psum_pool(name="spread_sums", bufs=2) as spread_sums:
-            for dest, first_mix, count in ((step_all, STEP, 4), (low_23, LOW + 2, 2)):
-                for j in range(count):
+            for dest, first_mix, order in ((step_all, STEP, (0, 1, 2, 3)), (low_23, LOW + 2, (1, 0))):
+                for j in order:
                     spread_sum = spread_sums.tile([P, H], F32, name="spread_sum")
                     accumulate(spread_sum, spread[:, first_mix + j, :], tables, start=True, stop=True)
                     copy_out(dest[:, j * H : (j + 1) * H], spread_sum)
@@ -88,7 +87,7 @@ def tile_dwnmodel_kernel(tc, x, thr, luts, offs, out):
                 return bits[:].indirect(offsets[:, fold * PIECE : (fold + 1) * PIECE])
 
             def folds_1_and_2(block):
-                x_block = work.tile([P, S], F32, name="x_block")
+                x_block = loaded.tile([P, S], F32, name="x_block")
                 bits = work.tile([P, S], F32, name="bits")
                 for half in range(2):
                     cols = slice(half * HALF, (half + 1) * HALF)
@@ -107,27 +106,30 @@ def tile_dwnmodel_kernel(tc, x, thr, luts, offs, out):
                 accumulate(out_sum, spread[:, LOW, :], tables, start=True)
                 accumulate(out_sum, plus[:], p[:, 0:H])
 
-                a_diff = work.tile([P, 2 * H], F32, name="a_diff")
-                nc.vector.tensor_add(a_diff[:], p[:, 2 * H : 4 * H], low_23[:])
+                upper = work.tile([P, 2 * H], F32, name="upper")
                 q = work.tile([P, 2 * H], F32, name="q")
                 for e in (1, 0):
                     part = slice(e * H, (e + 1) * H)
-                    nc.vector.tensor_tensor(q[:, part], picked(bits, 1), a_diff[:, part], ALU.mult)
+                    nc.vector.tensor_add(upper[:, part], p[:, (2 + e) * H : (3 + e) * H], low_23[:, part])
+                    nc.vector.tensor_tensor(q[:, part], picked(bits, 1), upper[:, part], ALU.mult)
 
-                accumulate(b_diff_sum, plus[:], q[:, H : 2 * H])
-                accumulate(b_diff_sum, minus[:], q[:, 0:H], stop=True)
-                accumulate(out_sum, plus[:], q[:, 0:H])
+                accumulate(b_diff_sum, plus[:], q[:, H : 2 * H], stop=True)
                 b_diff = work.tile([P, H], F32, name="b_diff")
                 copy_out(b_diff, b_diff_sum)
+                accumulate(out_sum, plus[:], q[:, 0:H])
                 return bits, b_diff, out_sum
 
             def fold_3(block, bits, b_diff, out_sum):
                 s = work.tile([P, H], F32, name="s")
-                nc.vector.tensor_tensor(s[:], picked(bits, 2), b_diff[:], ALU.mult)
-                accumulate(out_sum, plus[:], s, stop=True)
                 result = work.tile([P, H], F32, name="result")
-                copy_out(result, out_sum)
-                nc.scalar.dma_start(out[block * P : (block + 1) * P, :], result[:])
+                for bank in range(H // BANK):
+                    cols = slice(bank * BANK, (bank + 1) * BANK)
+                    first = 2 * PIECE + bank * (BANK // 16)
+                    picked_bank = bits[:].indirect(offsets[:, first : first + BANK // 16])
+                    nc.vector.tensor_tensor(s[:, cols], picked_bank, b_diff[:, cols], ALU.mult)
+                    nc.tensor.matmul(out_sum[:, cols], plus[:], s[:, cols], start=False, stop=True)
+                    nc.scalar.copy(result[:, cols], out_sum[:, cols])
+                    nc.scalar.dma_start(out[block * P : (block + 1) * P, cols], result[:, cols])
 
             blocks = C // P
             waiting = folds_1_and_2(0)

@@ -11,29 +11,32 @@ S = 2048
 HALF = S // 2
 H = 1024
 E = 8
-PIECE = H // 16
+FOLDS = 3
+COMBOS = E // 2
 BANK = 512
 
 LOW = 0
-HIGH = 4
-STEP = 8
-MIXES = 12
+HIGH = COMBOS
+STEP = 2 * COMBOS
+MIXES = 3 * COMBOS
+
+WORK_SETS = 3
 
 
 def tile_dwnmodel_kernel(tc, x, thr, luts, offs, out):
     nc = tc.nc
     with (
         tc.tile_pool(name="held", bufs=1) as held,
-        tc.tile_pool(name="loaded", bufs=1) as loaded,
-        tc.tile_pool(name="work", bufs=3) as work,
+        tc.tile_pool(name="work", bufs=WORK_SETS) as work,
     ):
         tables = held.tile([P, H], F32, name="tables")
-        for first, queue in ((0, nc.sync), (E, nc.scalar), (2 * E, nc.sync), (3 * E, nc.scalar)):
-            queue.dma_start(tables[first : first + E, :], luts)
+        for repeat in range(32 // E):
+            queue = (nc.sync, nc.scalar)[repeat % 2]
+            queue.dma_start(tables[repeat * E : (repeat + 1) * E, :], luts)
         nc.vector.memset(tables[32:64, :], 0.0)
         nc.vector.memset(tables[64:128, :], 0.0)
 
-        offsets = held.tile([P, 3 * PIECE], U16, name="offsets")
+        offsets = held.tile([P, FOLDS * H // 16], U16, name="offsets")
         nc.sync.dma_start(offsets[:], offs)
 
         thr_all = held.tile([P, S], F32, name="thr_all")
@@ -51,12 +54,14 @@ def tile_dwnmodel_kernel(tc, x, thr, luts, offs, out):
         nc.gpsimd.tensor_sub(ones[:, :, 1:2], ones[:, :, 1:2], ones[:, :, 0:1])
         twos = mix[:, 0:E].rearrange("k (rest two one) -> k rest two one", two=2, one=2)
         nc.gpsimd.tensor_sub(twos[:, :, 1:2, :], twos[:, :, 1:2, :], twos[:, :, 0:1, :])
-        nc.gpsimd.tensor_sub(mix[:, STEP : STEP + 4], mix[:, HIGH : HIGH + 4], mix[:, LOW : LOW + 4])
+        nc.gpsimd.tensor_sub(
+            mix[:, STEP : STEP + COMBOS], mix[:, HIGH : HIGH + COMBOS], mix[:, LOW : LOW + COMBOS]
+        )
         spread = held.tile([P, MIXES, P], F32, name="spread")
         for group in (STEP, LOW):
             nc.gpsimd.tensor_copy(
-                spread[:, group : group + 4, :],
-                mix[:, group : group + 4].unsqueeze(2).to_broadcast([P, 4, P]),
+                spread[:, group : group + COMBOS, :],
+                mix[:, group : group + COMBOS].unsqueeze(2).to_broadcast([P, COMBOS, P]),
             )
 
         def accumulate(total, weights, term, start=False, stop=False):
@@ -69,10 +74,10 @@ def tile_dwnmodel_kernel(tc, x, thr, luts, offs, out):
                 cols = slice(bank * BANK, (bank + 1) * BANK)
                 nc.scalar.copy(dest[:, cols], total[:, cols])
 
-        step_all = held.tile([P, 4 * H], F32, name="step_all")
+        step_all = held.tile([P, COMBOS * H], F32, name="step_all")
         low_23 = held.tile([P, 2 * H], F32, name="low_23")
         with tc.psum_pool(name="spread_sums", bufs=2) as spread_sums:
-            for dest, first_mix, order in ((step_all, STEP, (0, 1, 2, 3)), (low_23, LOW + 2, (1, 0))):
+            for dest, first_mix, order in ((step_all, STEP, range(COMBOS)), (low_23, LOW + 2, (1, 0))):
                 for j in order:
                     spread_sum = spread_sums.tile([P, H], F32, name="spread_sum")
                     accumulate(spread_sum, spread[:, first_mix + j, :], tables, start=True, stop=True)
@@ -83,21 +88,21 @@ def tile_dwnmodel_kernel(tc, x, thr, luts, offs, out):
             tc.psum_pool(name="out_sums", bufs=2) as out_sums,
         ):
 
-            def picked(bits, fold):
-                return bits[:].indirect(offsets[:, fold * PIECE : (fold + 1) * PIECE])
+            def picked(bits, entry, count):
+                return bits[:].indirect(offsets[:, entry // 16 : (entry + count) // 16])
 
             def folds_1_and_2(block):
-                x_block = loaded.tile([P, S], F32, name="x_block")
+                x_block = work.tile([P, S], F32, name="x_block")
                 bits = work.tile([P, S], F32, name="bits")
                 for half in range(2):
                     cols = slice(half * HALF, (half + 1) * HALF)
                     nc.sync.dma_start(x_block[:, cols], x[block * P : (block + 1) * P, cols])
                     nc.vector.tensor_tensor(bits[:, cols], x_block[:, cols], thr_all[:, cols], ALU.is_gt)
 
-                p = work.tile([P, 4 * H], F32, name="p")
-                for j in range(4):
+                p = work.tile([P, COMBOS * H], F32, name="p")
+                for j in range(COMBOS):
                     part = slice(j * H, (j + 1) * H)
-                    nc.vector.tensor_tensor(p[:, part], picked(bits, 0), step_all[:, part], ALU.mult)
+                    nc.vector.tensor_tensor(p[:, part], picked(bits, 0, H), step_all[:, part], ALU.mult)
 
                 b_diff_sum = diff_sums.tile([P, H], F32, name="b_diff_sum")
                 accumulate(b_diff_sum, spread[:, LOW + 1, :], tables, start=True)
@@ -111,7 +116,7 @@ def tile_dwnmodel_kernel(tc, x, thr, luts, offs, out):
                 for e in (1, 0):
                     part = slice(e * H, (e + 1) * H)
                     nc.vector.tensor_add(upper[:, part], p[:, (2 + e) * H : (3 + e) * H], low_23[:, part])
-                    nc.vector.tensor_tensor(q[:, part], picked(bits, 1), upper[:, part], ALU.mult)
+                    nc.vector.tensor_tensor(q[:, part], picked(bits, H, H), upper[:, part], ALU.mult)
 
                 accumulate(b_diff_sum, plus[:], q[:, H : 2 * H], stop=True)
                 b_diff = work.tile([P, H], F32, name="b_diff")
@@ -124,8 +129,7 @@ def tile_dwnmodel_kernel(tc, x, thr, luts, offs, out):
                 result = work.tile([P, H], F32, name="result")
                 for bank in range(H // BANK):
                     cols = slice(bank * BANK, (bank + 1) * BANK)
-                    first = 2 * PIECE + bank * (BANK // 16)
-                    picked_bank = bits[:].indirect(offsets[:, first : first + BANK // 16])
+                    picked_bank = picked(bits, 2 * H + bank * BANK, BANK)
                     nc.vector.tensor_tensor(s[:, cols], picked_bank, b_diff[:, cols], ALU.mult)
                     nc.tensor.matmul(out_sum[:, cols], plus[:], s[:, cols], start=False, stop=True)
                     nc.scalar.copy(result[:, cols], out_sum[:, cols])

@@ -77,11 +77,17 @@ def tile_dwnmodel_kernel(tc, x, thr, luts, offs, out):
         step_all = held.tile([P, COMBOS * H], F32, name="step_all")
         low_23 = held.tile([P, 2 * H], F32, name="low_23")
         with tc.psum_pool(name="spread_sums", bufs=2) as spread_sums:
-            for dest, first_mix, order in ((step_all, STEP, range(COMBOS)), (low_23, LOW + 2, (1, 0))):
-                for j in order:
-                    spread_sum = spread_sums.tile([P, H], F32, name="spread_sum")
-                    accumulate(spread_sum, spread[:, first_mix + j, :], tables, start=True, stop=True)
-                    copy_out(dest[:, j * H : (j + 1) * H], spread_sum)
+            for dest, first_mix, j in (
+                (step_all, STEP, 3),
+                (step_all, STEP, 1),
+                (low_23, LOW + 2, 1),
+                (step_all, STEP, 2),
+                (step_all, STEP, 0),
+                (low_23, LOW + 2, 0),
+            ):
+                spread_sum = spread_sums.tile([P, H], F32, name="spread_sum")
+                accumulate(spread_sum, spread[:, first_mix + j, :], tables, start=True, stop=True)
+                copy_out(dest[:, j * H : (j + 1) * H], spread_sum)
 
         with (
             tc.psum_pool(name="diff_sums", bufs=2) as diff_sums,
@@ -90,6 +96,8 @@ def tile_dwnmodel_kernel(tc, x, thr, luts, offs, out):
 
             def picked(bits, entry, count):
                 return bits[:].indirect(offsets[:, entry // 16 : (entry + count) // 16])
+
+            blocks = C // P
 
             def folds_1_and_2(block):
                 x_block = work.tile([P, S], F32, name="x_block")
@@ -100,28 +108,35 @@ def tile_dwnmodel_kernel(tc, x, thr, luts, offs, out):
                     nc.vector.tensor_tensor(bits[:, cols], x_block[:, cols], thr_all[:, cols], ALU.is_gt)
 
                 p = work.tile([P, COMBOS * H], F32, name="p")
-                for j in range(COMBOS):
+                upper = work.tile([P, 2 * H], F32, name="upper")
+                q = work.tile([P, 2 * H], F32, name="q")
+
+                def fold_1(j):
                     part = slice(j * H, (j + 1) * H)
                     nc.vector.tensor_tensor(p[:, part], picked(bits, 0, H), step_all[:, part], ALU.mult)
 
-                b_diff_sum = diff_sums.tile([P, H], F32, name="b_diff_sum")
-                accumulate(b_diff_sum, spread[:, LOW + 1, :], tables, start=True)
-                accumulate(b_diff_sum, plus[:], p[:, H : 2 * H])
-                out_sum = out_sums.tile([P, H], F32, name="out_sum")
-                accumulate(out_sum, spread[:, LOW, :], tables, start=True)
-                accumulate(out_sum, plus[:], p[:, 0:H])
-
-                upper = work.tile([P, 2 * H], F32, name="upper")
-                q = work.tile([P, 2 * H], F32, name="q")
-                for e in (1, 0):
+                def fold_2(e):
                     part = slice(e * H, (e + 1) * H)
                     nc.vector.tensor_add(upper[:, part], p[:, (2 + e) * H : (3 + e) * H], low_23[:, part])
                     nc.vector.tensor_tensor(q[:, part], picked(bits, H, H), upper[:, part], ALU.mult)
 
+                fold_1(3)
+                fold_1(1)
+                b_diff_sum = diff_sums.tile([P, H], F32, name="b_diff_sum")
+                accumulate(b_diff_sum, spread[:, LOW + 1, :], tables, start=True)
+                accumulate(b_diff_sum, plus[:], p[:, H : 2 * H])
+                fold_2(1)
                 accumulate(b_diff_sum, plus[:], q[:, H : 2 * H], stop=True)
                 b_diff = work.tile([P, H], F32, name="b_diff")
                 copy_out(b_diff, b_diff_sum)
-                accumulate(out_sum, plus[:], q[:, 0:H])
+
+                fold_1(2)
+                fold_1(0)
+                out_sum = out_sums.tile([P, H], F32, name="out_sum")
+                accumulate(out_sum, spread[:, LOW, :], tables, start=True)
+                accumulate(out_sum, plus[:], p[:, 0:H])
+                fold_2(0)
+                accumulate(out_sum, plus[:], q[:, 0:H], stop=(block == blocks - 1))
                 return bits, b_diff, out_sum
 
             def fold_3(block, bits, b_diff, out_sum):
@@ -131,11 +146,13 @@ def tile_dwnmodel_kernel(tc, x, thr, luts, offs, out):
                     cols = slice(bank * BANK, (bank + 1) * BANK)
                     picked_bank = picked(bits, 2 * H + bank * BANK, BANK)
                     nc.vector.tensor_tensor(s[:, cols], picked_bank, b_diff[:, cols], ALU.mult)
-                    nc.tensor.matmul(out_sum[:, cols], plus[:], s[:, cols], start=False, stop=True)
-                    nc.scalar.copy(result[:, cols], out_sum[:, cols])
+                    if block < blocks - 1:
+                        nc.tensor.matmul(out_sum[:, cols], plus[:], s[:, cols], start=False, stop=True)
+                        nc.scalar.copy(result[:, cols], out_sum[:, cols])
+                    else:
+                        nc.vector.tensor_add(result[:, cols], out_sum[:, cols], s[:, cols])
                     nc.scalar.dma_start(out[block * P : (block + 1) * P, cols], result[:, cols])
 
-            blocks = C // P
             waiting = folds_1_and_2(0)
             for block in range(1, blocks):
                 following = folds_1_and_2(block)

@@ -2,8 +2,10 @@ import concourse.mybir as mybir
 from concourse.masks import make_identity
 
 F32 = mybir.dt.float32
+BF16 = mybir.dt.bfloat16
 U16 = mybir.dt.uint16
 ALU = mybir.AluOpType
+ACT = mybir.ActivationFunctionType
 
 P = 128
 C = 512
@@ -12,6 +14,7 @@ HALF = S // 2
 H = 1024
 E = 8
 FOLDS = 3
+FLIPS = S // P
 COMBOS = E // 2
 BANK = 512
 
@@ -45,6 +48,16 @@ def tile_dwnmodel_kernel(tc, x, thr, luts, offs, out):
             cols = slice(half * HALF, (half + 1) * HALF)
             nc.scalar.dma_start(thr_all[:, cols], thr_row[cols].partition_broadcast(P))
 
+        x_blocks = []
+        for block in range(C // P):
+            x_block = work.tile([P, S], F32, name="x_block")
+            for half in range(2):
+                cols = slice(half * HALF, (half + 1) * HALF)
+                nc.sync.dma_start(x_block[:, cols], x[block * P : (block + 1) * P, cols])
+            x_blocks.append(x_block)
+        thr_column = held.tile([P, FLIPS], F32, name="thr_column")
+        nc.sync.dma_start(thr_column[:], thr.rearrange("one (f p) -> p (one f)", p=P))
+
         plus = held.tile([P, P], F32, name="plus")
         make_identity(nc, plus[:])
 
@@ -63,6 +76,9 @@ def tile_dwnmodel_kernel(tc, x, thr, luts, offs, out):
                 spread[:, group : group + COMBOS, :],
                 mix[:, group : group + COMBOS].unsqueeze(2).to_broadcast([P, COMBOS, P]),
             )
+
+        plus_bf16 = held.tile([P, P], BF16, name="plus_bf16")
+        nc.gpsimd.tensor_copy(plus_bf16[:], plus[:])
 
         def accumulate(total, weights, term, start=False, stop=False):
             for bank in range(H // BANK):
@@ -90,7 +106,8 @@ def tile_dwnmodel_kernel(tc, x, thr, luts, offs, out):
                 copy_out(dest[:, j * H : (j + 1) * H], spread_sum)
 
         with (
-            tc.psum_pool(name="diff_sums", bufs=2) as diff_sums,
+            tc.psum_pool(name="flips", bufs=2) as flips,
+            tc.psum_pool(name="diff_sums", bufs=1) as diff_sums,
             tc.psum_pool(name="out_sums", bufs=2) as out_sums,
         ):
 
@@ -99,33 +116,35 @@ def tile_dwnmodel_kernel(tc, x, thr, luts, offs, out):
 
             blocks = C // P
 
-            def folds_1_and_2(block):
-                x_block = work.tile([P, S], F32, name="x_block")
-                bits = work.tile([P, S], F32, name="bits")
-                for half in range(2):
-                    cols = slice(half * HALF, (half + 1) * HALF)
-                    nc.sync.dma_start(x_block[:, cols], x[block * P : (block + 1) * P, cols])
-                    nc.vector.tensor_tensor(bits[:, cols], x_block[:, cols], thr_all[:, cols], ALU.is_gt)
+            def folds_1_and_2(block, waiting):
+                last = block == blocks - 1
+                bits = all_bits[block]
 
                 p = work.tile([P, COMBOS * H], F32, name="p")
-                upper = work.tile([P, 2 * H], F32, name="upper")
+                a_3 = work.tile([P, H], F32, name="a_3")
+                a_2 = waiting[1] if last else work.tile([P, H], F32, name="a_2")
+                upper = (a_2, a_3)
                 q = work.tile([P, 2 * H], F32, name="q")
 
                 def fold_1(j):
                     part = slice(j * H, (j + 1) * H)
                     nc.vector.tensor_tensor(p[:, part], picked(bits, 0, H), step_all[:, part], ALU.mult)
 
-                def fold_2(e):
+                def fold_2(e, width):
                     part = slice(e * H, (e + 1) * H)
-                    nc.vector.tensor_add(upper[:, part], p[:, (2 + e) * H : (3 + e) * H], low_23[:, part])
-                    nc.vector.tensor_tensor(q[:, part], picked(bits, H, H), upper[:, part], ALU.mult)
+                    nc.vector.tensor_add(upper[e][:], p[:, (2 + e) * H : (3 + e) * H], low_23[:, part])
+                    for first in range(0, H, width):
+                        cols = slice(e * H + first, e * H + first + width)
+                        picked_part = picked(bits, H + first, width)
+                        factor = upper[e][:, first : first + width]
+                        nc.vector.tensor_tensor(q[:, cols], picked_part, factor, ALU.mult)
 
                 fold_1(3)
                 fold_1(1)
                 b_diff_sum = diff_sums.tile([P, H], F32, name="b_diff_sum")
                 accumulate(b_diff_sum, spread[:, LOW + 1, :], tables, start=True)
                 accumulate(b_diff_sum, plus[:], p[:, H : 2 * H])
-                fold_2(1)
+                fold_2(1, H)
                 accumulate(b_diff_sum, plus[:], q[:, H : 2 * H], stop=True)
                 b_diff = work.tile([P, H], F32, name="b_diff")
                 copy_out(b_diff, b_diff_sum)
@@ -135,17 +154,22 @@ def tile_dwnmodel_kernel(tc, x, thr, luts, offs, out):
                 out_sum = out_sums.tile([P, H], F32, name="out_sum")
                 accumulate(out_sum, spread[:, LOW, :], tables, start=True)
                 accumulate(out_sum, plus[:], p[:, 0:H])
-                fold_2(0)
-                accumulate(out_sum, plus[:], q[:, 0:H], stop=(block == blocks - 1))
+                if last:
+                    fold_3(block - 1, *waiting)
+                fold_2(0, BANK if last else H)
+                accumulate(out_sum, plus[:], q[:, 0:H], stop=last)
+                if waiting and not last:
+                    fold_3(block - 1, *waiting)
                 return bits, b_diff, out_sum
 
             def fold_3(block, bits, b_diff, out_sum):
                 s = work.tile([P, H], F32, name="s")
                 result = work.tile([P, H], F32, name="result")
-                for bank in range(H // BANK):
-                    cols = slice(bank * BANK, (bank + 1) * BANK)
-                    picked_bank = picked(bits, 2 * H + bank * BANK, BANK)
+                banks = [slice(bank * BANK, (bank + 1) * BANK) for bank in range(H // BANK)]
+                for cols in banks:
+                    picked_bank = picked(bits, 2 * H + cols.start, BANK)
                     nc.vector.tensor_tensor(s[:, cols], picked_bank, b_diff[:, cols], ALU.mult)
+                for cols in banks:
                     if block < blocks - 1:
                         nc.tensor.matmul(out_sum[:, cols], plus[:], s[:, cols], start=False, stop=True)
                         nc.scalar.copy(result[:, cols], out_sum[:, cols])
@@ -153,9 +177,43 @@ def tile_dwnmodel_kernel(tc, x, thr, luts, offs, out):
                         nc.vector.tensor_add(result[:, cols], out_sum[:, cols], s[:, cols])
                     nc.scalar.dma_start(out[block * P : (block + 1) * P, cols], result[:, cols])
 
-            waiting = folds_1_and_2(0)
-            for block in range(1, blocks):
-                following = folds_1_and_2(block)
-                fold_3(block - 1, *waiting)
-                waiting = following
+            all_bits = {}
+
+            def compare(block):
+                bits = work.tile([P, S], F32, name="bits")
+                for half in range(2):
+                    cols = slice(half * HALF, (half + 1) * HALF)
+                    nc.vector.tensor_tensor(bits[:, cols], x_blocks[block][:, cols], thr_all[:, cols], ALU.is_gt)
+                all_bits[block] = bits
+
+            def signs_of(pair):
+                signs = work.tile([P, FLIPS, len(pair) * P], BF16, name="signs", bufs=1)
+                for f in range(FLIPS):
+                    flip = flips.tile([P, BANK], F32, name="flip")
+                    for i, block in enumerate(pair):
+                        square = x_blocks[block][:, f * P : (f + 1) * P]
+                        nc.tensor.transpose(flip[:, i * P : (i + 1) * P], square, plus[:])
+                    used = flip[:, 0 : len(pair) * P]
+                    nc.scalar.activation(signs[:, f, :], used, ACT.Sign, bias=thr_column[:, f : f + 1], scale=-1.0)
+                return signs
+
+            def bits_of(signs, i, block):
+                bits = work.tile([P, S], F32, name="bits")
+                for bank in range(S // BANK):
+                    flip = flips.tile([P, BANK], F32, name="flip")
+                    for k in range(BANK // P):
+                        square = signs[:, bank * (BANK // P) + k, i * P : (i + 1) * P]
+                        nc.tensor.matmul(flip[:, k * P : (k + 1) * P], square, plus_bf16[:], start=True, stop=True)
+                    nc.scalar.activation(bits[:, bank * BANK : (bank + 1) * BANK], flip[:], ACT.Relu, scale=-1.0)
+                all_bits[block] = bits
+
+            compare(0)
+            compare(1)
+            signs = signs_of((2, 3))
+            bits_of(signs, 0, 2)
+            waiting = ()
+            for block in range(blocks):
+                waiting = folds_1_and_2(block, waiting)
+                if block == 1:
+                    bits_of(signs, 1, 3)
             fold_3(blocks - 1, *waiting)

@@ -16,6 +16,7 @@ E = 8
 FOLDS = 3
 FLIPS = S // P
 COMBOS = E // 2
+ROWS = H // P
 BANK = 512
 
 LOW = 0
@@ -32,68 +33,63 @@ def tile_dwnmodel_kernel(tc, x, thr, luts, offs, out):
         tc.tile_pool(name="held", bufs=1) as held,
         tc.tile_pool(name="work", bufs=WORK_SETS) as work,
     ):
-        tables = held.tile([P, H], F32, name="tables")
-        for repeat in range(32 // E):
-            queue = (nc.sync, nc.scalar)[repeat % 2]
-            queue.dma_start(tables[repeat * E : (repeat + 1) * E, :], luts)
-        nc.vector.memset(tables[32:64, :], 0.0)
-        nc.vector.memset(tables[64:128, :], 0.0)
-
-        offsets = held.tile([P, FOLDS * H // 16], U16, name="offsets")
-        nc.sync.dma_start(offsets[:], offs)
+        tables = held.tile([E * ROWS, P], F32, name="tables")
+        nc.sync.dma_start(tables[:], luts.rearrange("e (a p) -> (e a) p", p=P))
 
         thr_all = held.tile([P, S], F32, name="thr_all")
         thr_row = thr.rearrange("one s -> (one s)")
-        for half in range(2):
-            cols = slice(half * HALF, (half + 1) * HALF)
-            nc.scalar.dma_start(thr_all[:, cols], thr_row[cols].partition_broadcast(P))
-
-        x_blocks = []
-        for block in range(C // P):
-            x_block = work.tile([P, S], F32, name="x_block")
-            for half in range(2):
-                cols = slice(half * HALF, (half + 1) * HALF)
-                nc.sync.dma_start(x_block[:, cols], x[block * P : (block + 1) * P, cols])
-            x_blocks.append(x_block)
+        x_blocks = [work.tile([P, S], F32, name="x_block") for block in range(C // P)]
+        offsets = held.tile([P, FOLDS * H // 16], U16, name="offsets")
+        halves = [slice(half * HALF, (half + 1) * HALF) for half in range(2)]
+        for cols in halves:
+            nc.sync.dma_start(thr_all[:, cols], thr_row[cols].partition_broadcast(P))
+            nc.sync.dma_start(x_blocks[0][:, cols], x[0:P, cols])
+        nc.sync.dma_start(offsets[:], offs)
+        for block in range(1, C // P):
+            for cols in halves:
+                nc.sync.dma_start(x_blocks[block][:, cols], x[block * P : (block + 1) * P, cols])
         thr_column = held.tile([P, FLIPS], F32, name="thr_column")
         nc.sync.dma_start(thr_column[:], thr.rearrange("one (f p) -> p (one f)", p=P))
 
         plus = held.tile([P, P], F32, name="plus")
         make_identity(nc, plus[:])
-
-        mix = held.tile([P, MIXES], F32, name="mix")
-        nc.gpsimd.tensor_copy(mix[:, 0:E], plus[:, 0:E])
-        ones = mix[:, 0:E].rearrange("k (rest one) -> k rest one", one=2)
-        nc.gpsimd.tensor_sub(ones[:, :, 1:2], ones[:, :, 1:2], ones[:, :, 0:1])
-        twos = mix[:, 0:E].rearrange("k (rest two one) -> k rest two one", two=2, one=2)
-        nc.gpsimd.tensor_sub(twos[:, :, 1:2, :], twos[:, :, 1:2, :], twos[:, :, 0:1, :])
-        nc.gpsimd.tensor_sub(
-            mix[:, STEP : STEP + COMBOS], mix[:, HIGH : HIGH + COMBOS], mix[:, LOW : LOW + COMBOS]
-        )
-        spread = held.tile([P, MIXES, P], F32, name="spread")
-        for group in (STEP, LOW):
-            nc.gpsimd.tensor_copy(
-                spread[:, group : group + COMBOS, :],
-                mix[:, group : group + COMBOS].unsqueeze(2).to_broadcast([P, COMBOS, P]),
-            )
-
         plus_bf16 = held.tile([P, P], BF16, name="plus_bf16")
         nc.gpsimd.tensor_copy(plus_bf16[:], plus[:])
 
-        def accumulate(total, weights, term, start=False, stop=False):
+        def accumulate(total, term, stop=False):
             for bank in range(H // BANK):
                 cols = slice(bank * BANK, (bank + 1) * BANK)
-                nc.tensor.matmul(total[:, cols], weights, term[:, cols], start=start, stop=stop)
+                nc.tensor.matmul(total[:, cols], plus[:], term[:, cols], start=False, stop=stop)
 
         def copy_out(dest, total):
             for bank in range(H // BANK):
                 cols = slice(bank * BANK, (bank + 1) * BANK)
                 nc.scalar.copy(dest[:, cols], total[:, cols])
 
+        combos = held.tile([P, MIXES, ROWS], F32, name="combos")
+        with tc.psum_pool(name="table_flips", bufs=1) as table_flips:
+            table_flip = table_flips.tile([P, E * ROWS], F32, name="table_flip")
+            nc.tensor.transpose(table_flip[:], tables[:], plus[0 : E * ROWS, 0 : E * ROWS])
+            nc.scalar.copy(combos[:, 0:E, :], table_flip[:].rearrange("p (e a) -> p e a", e=E))
+        ones = combos[:, 0:E, :].rearrange("p (rest one) a -> p rest one a", one=2)
+        nc.gpsimd.tensor_sub(ones[:, :, 1:2, :], ones[:, :, 1:2, :], ones[:, :, 0:1, :])
+        twos = combos[:, 0:E, :].rearrange("p (rest two one) a -> p rest two (one a)", two=2, one=2)
+        nc.gpsimd.tensor_sub(twos[:, :, 1:2, :], twos[:, :, 1:2, :], twos[:, :, 0:1, :])
+        nc.gpsimd.tensor_sub(
+            combos[:, STEP : STEP + COMBOS, :], combos[:, HIGH : HIGH + COMBOS, :], combos[:, LOW : LOW + COMBOS, :]
+        )
+
+        def spread(total, combo, alone):
+            for a in range(ROWS):
+                column = combos[:, combo, a : a + 1].to_broadcast([P, P])
+                square = total[:, a * P : (a + 1) * P]
+                start = alone or a % (BANK // P) == 0
+                nc.tensor.matmul(square, column, plus[:], start=start, stop=alone, is_transpose=True)
+
         step_all = held.tile([P, COMBOS * H], F32, name="step_all")
         low_23 = held.tile([P, 2 * H], F32, name="low_23")
         with tc.psum_pool(name="spread_sums", bufs=2) as spread_sums:
-            for dest, first_mix, j in (
+            for dest, first_combo, j in (
                 (step_all, STEP, 3),
                 (step_all, STEP, 1),
                 (low_23, LOW + 2, 1),
@@ -102,7 +98,7 @@ def tile_dwnmodel_kernel(tc, x, thr, luts, offs, out):
                 (low_23, LOW + 2, 0),
             ):
                 spread_sum = spread_sums.tile([P, H], F32, name="spread_sum")
-                accumulate(spread_sum, spread[:, first_mix + j, :], tables, start=True, stop=True)
+                spread(spread_sum, first_combo + j, alone=True)
                 copy_out(dest[:, j * H : (j + 1) * H], spread_sum)
 
         with (
@@ -142,22 +138,22 @@ def tile_dwnmodel_kernel(tc, x, thr, luts, offs, out):
                 fold_1(3)
                 fold_1(1)
                 b_diff_sum = diff_sums.tile([P, H], F32, name="b_diff_sum")
-                accumulate(b_diff_sum, spread[:, LOW + 1, :], tables, start=True)
-                accumulate(b_diff_sum, plus[:], p[:, H : 2 * H])
+                spread(b_diff_sum, LOW + 1, alone=False)
+                accumulate(b_diff_sum, p[:, H : 2 * H])
                 fold_2(1, H)
-                accumulate(b_diff_sum, plus[:], q[:, H : 2 * H], stop=True)
+                accumulate(b_diff_sum, q[:, H : 2 * H], stop=True)
                 b_diff = work.tile([P, H], F32, name="b_diff")
                 copy_out(b_diff, b_diff_sum)
 
                 fold_1(2)
                 fold_1(0)
                 out_sum = out_sums.tile([P, H], F32, name="out_sum")
-                accumulate(out_sum, spread[:, LOW, :], tables, start=True)
-                accumulate(out_sum, plus[:], p[:, 0:H])
+                spread(out_sum, LOW, alone=False)
+                accumulate(out_sum, p[:, 0:H])
                 if last:
                     fold_3(block - 1, *waiting)
                 fold_2(0, BANK if last else H)
-                accumulate(out_sum, plus[:], q[:, 0:H], stop=last)
+                accumulate(out_sum, q[:, 0:H], stop=last)
                 if waiting and not last:
                     fold_3(block - 1, *waiting)
                 return bits, b_diff, out_sum
@@ -181,8 +177,7 @@ def tile_dwnmodel_kernel(tc, x, thr, luts, offs, out):
 
             def compare(block):
                 bits = work.tile([P, S], F32, name="bits")
-                for half in range(2):
-                    cols = slice(half * HALF, (half + 1) * HALF)
+                for cols in halves:
                     nc.vector.tensor_tensor(bits[:, cols], x_blocks[block][:, cols], thr_all[:, cols], ALU.is_gt)
                 all_bits[block] = bits
 

@@ -18,11 +18,14 @@ FLIPS = S // P
 COMBOS = E // 2
 ROWS = H // P
 BANK = 512
+SQUARES = BANK // P
 
 LOW = 0
 HIGH = COMBOS
 STEP = 2 * COMBOS
 MIXES = 3 * COMBOS
+
+RING = 4
 
 WORK_SETS = 3
 
@@ -32,45 +35,49 @@ def tile_dwnmodel_kernel(tc, x, thr, luts, offs, out):
     with (
         tc.tile_pool(name="held", bufs=1) as held,
         tc.tile_pool(name="work", bufs=WORK_SETS) as work,
+        tc.tile_pool(name="products", bufs=RING) as products,
+        tc.psum_pool(name="flips", bufs=2) as flips,
+        tc.psum_pool(name="diff_sums", bufs=2) as diff_sums,
+        tc.psum_pool(name="out_sums", bufs=4) as out_sums,
     ):
         tables = held.tile([E * ROWS, P], F32, name="tables")
         nc.sync.dma_start(tables[:], luts.rearrange("e (a p) -> (e a) p", p=P))
 
         thr_all = held.tile([P, S], F32, name="thr_all")
         thr_row = thr.rearrange("one s -> (one s)")
-        x_blocks = [work.tile([P, S], F32, name="x_block") for block in range(C // P)]
+        x_blocks = [work.tile([P, S], F32, name="x_block", bufs=4) for block in range(C // P)]
         offsets = held.tile([P, FOLDS * H // 16], U16, name="offsets")
         halves = [slice(half * HALF, (half + 1) * HALF) for half in range(2)]
         for cols in halves:
             nc.sync.dma_start(thr_all[:, cols], thr_row[cols].partition_broadcast(P))
             nc.sync.dma_start(x_blocks[0][:, cols], x[0:P, cols])
         nc.sync.dma_start(offsets[:], offs)
+        thr_column = held.tile([P, FLIPS], F32, name="thr_column")
+        nc.sync.dma_start(thr_column[:], thr.rearrange("one (f p) -> p (one f)", p=P))
         for block in range(1, C // P):
             for cols in halves:
                 nc.sync.dma_start(x_blocks[block][:, cols], x[block * P : (block + 1) * P, cols])
-        thr_column = held.tile([P, FLIPS], F32, name="thr_column")
-        nc.sync.dma_start(thr_column[:], thr.rearrange("one (f p) -> p (one f)", p=P))
 
         plus = held.tile([P, P], F32, name="plus")
         make_identity(nc, plus[:])
         plus_bf16 = held.tile([P, P], BF16, name="plus_bf16")
         nc.gpsimd.tensor_copy(plus_bf16[:], plus[:])
 
-        def accumulate(total, term, stop=False):
-            for bank in range(H // BANK):
-                cols = slice(bank * BANK, (bank + 1) * BANK)
-                nc.tensor.matmul(total[:, cols], plus[:], term[:, cols], start=False, stop=stop)
+        banks = [slice(bank * BANK, (bank + 1) * BANK) for bank in range(H // BANK)]
+
+        def accumulate(total, term, start=False, stop=False):
+            for bank, cols in zip(total, banks):
+                nc.tensor.matmul(bank[:], plus[:], term[:, cols], start=start, stop=stop)
 
         def copy_out(dest, total):
-            for bank in range(H // BANK):
-                cols = slice(bank * BANK, (bank + 1) * BANK)
-                nc.scalar.copy(dest[:, cols], total[:, cols])
+            for bank, cols in zip(total, banks):
+                nc.scalar.copy(dest[:, cols], bank[:])
 
         combos = held.tile([P, MIXES, ROWS], F32, name="combos")
-        with tc.psum_pool(name="table_flips", bufs=1) as table_flips:
-            table_flip = table_flips.tile([P, E * ROWS], F32, name="table_flip")
-            nc.tensor.transpose(table_flip[:], tables[:], plus[0 : E * ROWS, 0 : E * ROWS])
-            nc.scalar.copy(combos[:, 0:E, :], table_flip[:].rearrange("p (e a) -> p e a", e=E))
+        flip = flips.tile([P, BANK], F32, name="total")
+        table_flip = flip[:, 0 : E * ROWS]
+        nc.tensor.transpose(table_flip, tables[:], plus[0 : E * ROWS, 0 : E * ROWS])
+        nc.scalar.copy(combos[:, 0:E, :], table_flip.rearrange("p (e a) -> p e a", e=E))
         ones = combos[:, 0:E, :].rearrange("p (rest one) a -> p rest one a", one=2)
         nc.gpsimd.tensor_sub(ones[:, :, 1:2, :], ones[:, :, 1:2, :], ones[:, :, 0:1, :])
         twos = combos[:, 0:E, :].rearrange("p (rest two one) a -> p rest two (one a)", two=2, one=2)
@@ -79,136 +86,154 @@ def tile_dwnmodel_kernel(tc, x, thr, luts, offs, out):
             combos[:, STEP : STEP + COMBOS, :], combos[:, HIGH : HIGH + COMBOS, :], combos[:, LOW : LOW + COMBOS, :]
         )
 
-        def spread(total, combo, alone):
-            for a in range(ROWS):
+        def spread(total, combo, bank, alone=False, last=False):
+            for square in range(SQUARES):
+                a = bank * SQUARES + square
                 column = combos[:, combo, a : a + 1].to_broadcast([P, P])
-                square = total[:, a * P : (a + 1) * P]
-                start = alone or a % (BANK // P) == 0
-                nc.tensor.matmul(square, column, plus[:], start=start, stop=alone, is_transpose=True)
+                cols = slice(square * P, (square + 1) * P)
+                stop = alone or (last and square == SQUARES - 1)
+                nc.tensor.matmul(total[:, cols], column, plus[:], start=alone, stop=stop, is_transpose=True)
+
+        def spread_all(dest, combo):
+            for bank, cols in enumerate(banks):
+                total = (flips, diff_sums)[bank].tile([P, BANK], F32, name="total")
+                spread(total, combo, bank, alone=True)
+                nc.scalar.copy(dest[:, cols], total[:])
 
         step_all = held.tile([P, COMBOS * H], F32, name="step_all")
-        low_23 = held.tile([P, 2 * H], F32, name="low_23")
-        with tc.psum_pool(name="spread_sums", bufs=2) as spread_sums:
-            for dest, first_combo, j in (
-                (step_all, STEP, 3),
-                (step_all, STEP, 1),
-                (low_23, LOW + 2, 1),
-                (step_all, STEP, 2),
-                (step_all, STEP, 0),
-                (low_23, LOW + 2, 0),
-            ):
-                spread_sum = spread_sums.tile([P, H], F32, name="spread_sum")
-                spread(spread_sum, first_combo + j, alone=True)
-                copy_out(dest[:, j * H : (j + 1) * H], spread_sum)
+        for j in (3, 2, 1, 0):
+            spread_all(step_all[:, j * H : (j + 1) * H], STEP + j)
 
-        with (
-            tc.psum_pool(name="flips", bufs=2) as flips,
-            tc.psum_pool(name="diff_sums", bufs=1) as diff_sums,
-            tc.psum_pool(name="out_sums", bufs=2) as out_sums,
-        ):
+        def picked(bits, entry, count):
+            return bits[:].indirect(offsets[:, entry // 16 : (entry + count) // 16])
 
-            def picked(bits, entry, count):
-                return bits[:].indirect(offsets[:, entry // 16 : (entry + count) // 16])
+        blocks = C // P
 
-            blocks = C // P
+        def picked_product(dest, bits, entry, factor):
+            count = dest.shape[1]
+            nc.vector.tensor_tensor(dest, picked(bits, entry, count), factor, ALU.mult)
 
-            def folds_1_and_2(block, waiting):
-                last = block == blocks - 1
-                bits = all_bits[block]
+        def product(block, p, j):
+            picked_product(p[:], all_bits[block], 0, step_all[:, j * H : (j + 1) * H])
 
-                p = work.tile([P, COMBOS * H], F32, name="p")
-                a_3 = work.tile([P, H], F32, name="a_3")
-                a_2 = waiting[1] if last else work.tile([P, H], F32, name="a_2")
-                upper = (a_2, a_3)
-                q = work.tile([P, 2 * H], F32, name="q")
+        def flip_squares(source, bank):
+            flip = flips.tile([P, BANK], F32, name="total")
+            for square in range(SQUARES):
+                a = bank * SQUARES + square
+                nc.tensor.transpose(flip[:, square * P : (square + 1) * P], source[:, a * P : (a + 1) * P], plus[:])
+            return flip
 
-                def fold_1(j):
-                    part = slice(j * H, (j + 1) * H)
-                    nc.vector.tensor_tensor(p[:, part], picked(bits, 0, H), step_all[:, part], ALU.mult)
+        def first_sums(block):
+            upper = work.tile([P, 2 * H], F32, name="upper")
+            for e in (1, 0):
+                p = products.tile([P, H], F32, name="product")
+                product(block, p, 2 + e)
+                flipped = work.tile([P, H], F32, name="flipped", bufs=2)
+                for bank in range(len(banks)):
+                    flip = flip_squares(p, bank)
+                    for square in range(SQUARES):
+                        a = bank * SQUARES + square
+                        bias = combos[:, LOW + 2 + e, a : a + 1]
+                        part = flip[:, square * P : (square + 1) * P]
+                        nc.scalar.activation(flipped[:, a * P : (a + 1) * P], part, ACT.Identity, bias=bias)
+                for bank, cols in enumerate(banks):
+                    flip = flip_squares(flipped, bank)
+                    nc.scalar.copy(upper[:, e * H + cols.start : e * H + cols.stop], flip[:])
+            return upper
 
-                def fold_2(e, width):
-                    part = slice(e * H, (e + 1) * H)
-                    nc.vector.tensor_add(upper[e][:], p[:, (2 + e) * H : (3 + e) * H], low_23[:, part])
-                    for first in range(0, H, width):
-                        cols = slice(e * H + first, e * H + first + width)
-                        picked_part = picked(bits, H + first, width)
-                        factor = upper[e][:, first : first + width]
-                        nc.vector.tensor_tensor(q[:, cols], picked_part, factor, ALU.mult)
+        def sum_of_two(block, e, upper, sums, stop):
+            p = products.tile([P, H], F32, name="product")
+            product(block, p, e)
+            total = [sums.tile([P, BANK], F32, name="total") for bank in banks]
+            accumulate(total, p, start=True)
+            for bank in range(len(banks)):
+                spread(total[bank], LOW + e, bank)
+            q = products.tile([P, H], F32, name="product")
+            picked_product(q[:], all_bits[block], H, upper[:, e * H : (e + 1) * H])
+            accumulate(total, q, stop=stop)
+            return total
 
-                fold_1(3)
-                fold_1(1)
-                b_diff_sum = diff_sums.tile([P, H], F32, name="b_diff_sum")
-                spread(b_diff_sum, LOW + 1, alone=False)
-                accumulate(b_diff_sum, p[:, H : 2 * H])
-                fold_2(1, H)
-                accumulate(b_diff_sum, q[:, H : 2 * H], stop=True)
-                b_diff = work.tile([P, H], F32, name="b_diff")
-                copy_out(b_diff, b_diff_sum)
+        def sum_b_diff(block, upper):
+            b_diff_sum = sum_of_two(block, 1, upper, diff_sums, stop=True)
+            b_diff = work.tile([P, H], F32, name="b_diff")
+            copy_out(b_diff, b_diff_sum)
+            return b_diff
 
-                fold_1(2)
-                fold_1(0)
-                out_sum = out_sums.tile([P, H], F32, name="out_sum")
-                spread(out_sum, LOW, alone=False)
-                accumulate(out_sum, p[:, 0:H])
-                if last:
-                    fold_3(block - 1, *waiting)
-                fold_2(0, BANK if last else H)
-                accumulate(out_sum, q[:, 0:H], stop=last)
-                if waiting and not last:
-                    fold_3(block - 1, *waiting)
-                return bits, b_diff, out_sum
+        def sum_out(block, upper):
+            return sum_of_two(block, 0, upper, out_sums, stop=block == blocks - 1)
 
-            def fold_3(block, bits, b_diff, out_sum):
-                s = work.tile([P, H], F32, name="s")
-                result = work.tile([P, H], F32, name="result")
-                banks = [slice(bank * BANK, (bank + 1) * BANK) for bank in range(H // BANK)]
-                for cols in banks:
-                    picked_bank = picked(bits, 2 * H + cols.start, BANK)
-                    nc.vector.tensor_tensor(s[:, cols], picked_bank, b_diff[:, cols], ALU.mult)
-                for cols in banks:
-                    if block < blocks - 1:
-                        nc.tensor.matmul(out_sum[:, cols], plus[:], s[:, cols], start=False, stop=True)
-                        nc.scalar.copy(result[:, cols], out_sum[:, cols])
-                    else:
-                        nc.vector.tensor_add(result[:, cols], out_sum[:, cols], s[:, cols])
-                    nc.scalar.dma_start(out[block * P : (block + 1) * P, cols], result[:, cols])
+        def second_sums(block, upper):
+            return sum_b_diff(block, upper), sum_out(block, upper)
 
-            all_bits = {}
+        def products_s(block, b_diff):
+            s = products.tile([P, H], F32, name="product")
+            for cols in banks:
+                picked_product(s[:, cols], all_bits[block], 2 * H + cols.start, b_diff[:, cols])
+            return s
 
-            def compare(block):
-                bits = work.tile([P, S], F32, name="bits")
-                for cols in halves:
-                    nc.vector.tensor_tensor(bits[:, cols], x_blocks[block][:, cols], thr_all[:, cols], ALU.is_gt)
-                all_bits[block] = bits
+        def store(block, result, cols):
+            nc.sync.dma_start(out[block * P : (block + 1) * P, cols], result[:, cols])
 
-            def signs_of(pair):
-                signs = work.tile([P, FLIPS, len(pair) * P], BF16, name="signs", bufs=1)
-                for f in range(FLIPS):
-                    flip = flips.tile([P, BANK], F32, name="flip")
+        def third_fold(block, b_diff, out_sum):
+            s = products_s(block, b_diff)
+            accumulate(out_sum, s, stop=True)
+            result = work.tile([P, H], F32, name="result", bufs=2)
+            for bank, cols in zip(out_sum, banks):
+                nc.scalar.copy(result[:, cols], bank[:])
+                store(block, result, cols)
+
+        all_bits = {}
+
+        def compare(block):
+            bits = work.tile([P, S], F32, name="bits", bufs=4)
+            for cols in halves:
+                nc.vector.tensor_tensor(bits[:, cols], x_blocks[block][:, cols], thr_all[:, cols], ALU.is_gt)
+            all_bits[block] = bits
+
+        def signs_of(pair):
+            signs = work.tile([P, FLIPS, len(pair) * P], BF16, name="signs", bufs=1)
+            width = len(pair) * P
+            for first in range(0, FLIPS, BANK // width):
+                total = diff_sums.tile([P, BANK], F32, name="total")
+                for k in range(BANK // width):
+                    f = first + k
                     for i, block in enumerate(pair):
                         square = x_blocks[block][:, f * P : (f + 1) * P]
-                        nc.tensor.transpose(flip[:, i * P : (i + 1) * P], square, plus[:])
-                    used = flip[:, 0 : len(pair) * P]
-                    nc.scalar.activation(signs[:, f, :], used, ACT.Sign, bias=thr_column[:, f : f + 1], scale=-1.0)
-                return signs
+                        nc.tensor.transpose(total[:, k * width + i * P : k * width + (i + 1) * P], square, plus[:])
+                    bias = thr_column[:, f : f + 1]
+                    part = total[:, k * width : (k + 1) * width]
+                    nc.scalar.activation(signs[:, f, :], part, ACT.Sign, bias=bias, scale=-1.0)
+            return signs
 
-            def bits_of(signs, i, block):
-                bits = work.tile([P, S], F32, name="bits")
-                for bank in range(S // BANK):
-                    flip = flips.tile([P, BANK], F32, name="flip")
-                    for k in range(BANK // P):
-                        square = signs[:, bank * (BANK // P) + k, i * P : (i + 1) * P]
-                        nc.tensor.matmul(flip[:, k * P : (k + 1) * P], square, plus_bf16[:], start=True, stop=True)
-                    nc.scalar.activation(bits[:, bank * BANK : (bank + 1) * BANK], flip[:], ACT.Relu, scale=-1.0)
-                all_bits[block] = bits
+        def bits_of(signs, i, block):
+            bits = work.tile([P, S], F32, name="bits", bufs=4)
+            for bank in range(S // BANK):
+                total = diff_sums.tile([P, BANK], F32, name="total")
+                for k in range(BANK // P):
+                    square = signs[:, bank * (BANK // P) + k, i * P : (i + 1) * P]
+                    nc.tensor.matmul(total[:, k * P : (k + 1) * P], square, plus_bf16[:], start=True, stop=True)
+                nc.scalar.activation(bits[:, bank * BANK : (bank + 1) * BANK], total[:], ACT.Relu, scale=-1.0)
+            all_bits[block] = bits
 
-            compare(0)
-            compare(1)
-            signs = signs_of((2, 3))
-            bits_of(signs, 0, 2)
-            waiting = ()
-            for block in range(blocks):
-                waiting = folds_1_and_2(block, waiting)
-                if block == 1:
-                    bits_of(signs, 1, 3)
-            fold_3(blocks - 1, *waiting)
+        compare(0)
+        signs = signs_of((2, 3))
+        bits_of(signs, 0, 2)
+        upper = {0: first_sums(0)}
+        compare(1)
+        upper[1] = first_sums(1)
+        ready = {0: second_sums(0, upper[0])}
+        bits_of(signs, 1, 3)
+        upper[2] = first_sums(2)
+        third_fold(0, *ready[0])
+        ready[1] = second_sums(1, upper[1])
+        upper[3] = first_sums(3)
+        third_fold(1, *ready[1])
+        ready[2] = second_sums(2, upper[2])
+        b_diff = sum_b_diff(3, upper[3])
+        third_fold(2, *ready[2])
+        out_sum = sum_out(3, upper[3])
+        s = products_s(3, b_diff)
+        result = work.tile([P, H], F32, name="result", bufs=2)
+        for bank, cols in zip(out_sum, banks):
+            nc.vector.tensor_add(result[:, cols], bank[:], s[:, cols])
+            store(3, result, cols)

@@ -10,7 +10,6 @@ ACT = mybir.ActivationFunctionType
 P = 128
 C = 512
 S = 2048
-HALF = S // 2
 H = 1024
 E = 8
 FOLDS = 3
@@ -40,23 +39,20 @@ def tile_dwnmodel_kernel(tc, x, thr, luts, offs, out):
         tc.psum_pool(name="diff_sums", bufs=2) as diff_sums,
         tc.psum_pool(name="out_sums", bufs=4) as out_sums,
     ):
-        tables = held.tile([E * ROWS, P], F32, name="tables")
-        nc.sync.dma_start(tables[:], luts.rearrange("e (a p) -> (e a) p", p=P))
+        by_row = held.tile([P, P], F32, name="by_row")
+        entries = E * ROWS
+        nc.vector.memset(by_row[entries:P, :], 0.0)
+        nc.sync.dma_start(by_row[0:entries, :], luts.rearrange("e (a p) -> (e a) p", p=P))
+        nc.sync.dma_start(by_row[entries : entries + FLIPS, :], thr.rearrange("one (f p) -> (one f) p", p=P))
 
-        thr_all = held.tile([P, S], F32, name="thr_all")
-        thr_row = thr.rearrange("one s -> (one s)")
         x_blocks = [work.tile([P, S], F32, name="x_block", bufs=4) for block in range(C // P)]
-        offsets = held.tile([P, FOLDS * H // 16], U16, name="offsets")
-        halves = [slice(half * HALF, (half + 1) * HALF) for half in range(2)]
-        for cols in halves:
-            nc.sync.dma_start(thr_all[:, cols], thr_row[cols].partition_broadcast(P))
+        x_banks = [slice(first, first + BANK) for first in range(0, S, BANK)]
+        for cols in x_banks:
             nc.sync.dma_start(x_blocks[0][:, cols], x[0:P, cols])
+        offsets = held.tile([P, FOLDS * H // 16], U16, name="offsets")
         nc.sync.dma_start(offsets[:], offs)
-        thr_column = held.tile([P, FLIPS], F32, name="thr_column")
-        nc.sync.dma_start(thr_column[:], thr.rearrange("one (f p) -> p (one f)", p=P))
         for block in range(1, C // P):
-            for cols in halves:
-                nc.sync.dma_start(x_blocks[block][:, cols], x[block * P : (block + 1) * P, cols])
+            nc.sync.dma_start(x_blocks[block][:], x[block * P : (block + 1) * P, :])
 
         plus = held.tile([P, P], F32, name="plus")
         make_identity(nc, plus[:])
@@ -75,9 +71,10 @@ def tile_dwnmodel_kernel(tc, x, thr, luts, offs, out):
 
         combos = held.tile([P, MIXES, ROWS], F32, name="combos")
         flip = flips.tile([P, BANK], F32, name="total")
-        table_flip = flip[:, 0 : E * ROWS]
-        nc.tensor.transpose(table_flip, tables[:], plus[0 : E * ROWS, 0 : E * ROWS])
-        nc.scalar.copy(combos[:, 0:E, :], table_flip.rearrange("p (e a) -> p e a", e=E))
+        nc.tensor.transpose(flip[:, 0:P], by_row[:], plus[:])
+        thr_column = held.tile([P, FLIPS], F32, name="thr_column")
+        nc.scalar.copy(thr_column[:], flip[:, entries : entries + FLIPS])
+        nc.scalar.copy(combos[:, 0:E, :], flip[:, 0:entries].rearrange("p (e a) -> p e a", e=E))
         ones = combos[:, 0:E, :].rearrange("p (rest one) a -> p rest one a", one=2)
         nc.gpsimd.tensor_sub(ones[:, :, 1:2, :], ones[:, :, 1:2, :], ones[:, :, 0:1, :])
         twos = combos[:, 0:E, :].rearrange("p (rest two one) a -> p rest two (one a)", two=2, one=2)
@@ -93,6 +90,12 @@ def tile_dwnmodel_kernel(tc, x, thr, luts, offs, out):
                 cols = slice(square * P, (square + 1) * P)
                 stop = alone or (last and square == SQUARES - 1)
                 nc.tensor.matmul(total[:, cols], column, plus[:], start=alone, stop=stop, is_transpose=True)
+
+        thr_banks = [out_sums.tile([P, BANK], F32, name="total") for cols in x_banks]
+        for f in range(FLIPS):
+            square = (f % SQUARES) * P
+            column = thr_column[:, f : f + 1].to_broadcast([P, P])
+            nc.tensor.transpose(thr_banks[f // SQUARES][:, square : square + P], column, plus[:])
 
         def spread_all(dest, combo):
             for bank, cols in enumerate(banks):
@@ -186,8 +189,8 @@ def tile_dwnmodel_kernel(tc, x, thr, luts, offs, out):
 
         def compare(block):
             bits = work.tile([P, S], F32, name="bits", bufs=4)
-            for cols in halves:
-                nc.vector.tensor_tensor(bits[:, cols], x_blocks[block][:, cols], thr_all[:, cols], ALU.is_gt)
+            for cols, thr_bank in zip(x_banks, thr_banks):
+                nc.vector.tensor_tensor(bits[:, cols], x_blocks[block][:, cols], thr_bank[:], ALU.is_gt)
             all_bits[block] = bits
 
         def signs_of(pair):

@@ -41,7 +41,7 @@ def tile_dwnmodel_kernel(tc, x, thr, luts, offs, out):
     ):
         by_row = held.tile([P, P], F32, name="by_row")
         entries = E * ROWS
-        nc.vector.memset(by_row[entries:P, :], 0.0)
+        nc.gpsimd.memset(by_row[entries:P, :], 0.0)
         nc.sync.dma_start(by_row[0:entries, :], luts.rearrange("e (a p) -> (e a) p", p=P))
         nc.sync.dma_start(by_row[entries : entries + FLIPS, :], thr.rearrange("one (f p) -> (one f) p", p=P))
 
@@ -65,10 +65,6 @@ def tile_dwnmodel_kernel(tc, x, thr, luts, offs, out):
             for bank, cols in zip(total, banks):
                 nc.tensor.matmul(bank[:], plus[:], term[:, cols], start=start, stop=stop)
 
-        def copy_out(dest, total):
-            for bank, cols in zip(total, banks):
-                nc.scalar.copy(dest[:, cols], bank[:])
-
         combos = held.tile([P, MIXES, ROWS], F32, name="combos")
         flip = flips.tile([P, BANK], F32, name="total")
         nc.tensor.transpose(flip[:, 0:P], by_row[:], plus[:])
@@ -76,36 +72,41 @@ def tile_dwnmodel_kernel(tc, x, thr, luts, offs, out):
         nc.scalar.copy(thr_column[:], flip[:, entries : entries + FLIPS])
         nc.scalar.copy(combos[:, 0:E, :], flip[:, 0:entries].rearrange("p (e a) -> p e a", e=E))
         ones = combos[:, 0:E, :].rearrange("p (rest one) a -> p rest one a", one=2)
-        nc.gpsimd.tensor_sub(ones[:, :, 1:2, :], ones[:, :, 1:2, :], ones[:, :, 0:1, :])
+        nc.vector.tensor_sub(ones[:, :, 1:2, :], ones[:, :, 1:2, :], ones[:, :, 0:1, :])
         twos = combos[:, 0:E, :].rearrange("p (rest two one) a -> p rest two (one a)", two=2, one=2)
-        nc.gpsimd.tensor_sub(twos[:, :, 1:2, :], twos[:, :, 1:2, :], twos[:, :, 0:1, :])
-        nc.gpsimd.tensor_sub(
+        nc.vector.tensor_sub(twos[:, :, 1:2, :], twos[:, :, 1:2, :], twos[:, :, 0:1, :])
+        nc.vector.tensor_sub(
             combos[:, STEP : STEP + COMBOS, :], combos[:, HIGH : HIGH + COMBOS, :], combos[:, LOW : LOW + COMBOS, :]
         )
 
-        def spread(total, combo, bank, alone=False, last=False):
+        def spread(total, combo, bank, alone=False):
             for square in range(SQUARES):
                 a = bank * SQUARES + square
                 column = combos[:, combo, a : a + 1].to_broadcast([P, P])
                 cols = slice(square * P, (square + 1) * P)
-                stop = alone or (last and square == SQUARES - 1)
-                nc.tensor.matmul(total[:, cols], column, plus[:], start=alone, stop=stop, is_transpose=True)
+                nc.tensor.matmul(total[:, cols], column, plus[:], start=alone, stop=alone, is_transpose=True)
 
         thr_banks = [out_sums.tile([P, BANK], F32, name="total") for cols in x_banks]
-        for f in range(FLIPS):
-            square = (f % SQUARES) * P
-            column = thr_column[:, f : f + 1].to_broadcast([P, P])
-            nc.tensor.transpose(thr_banks[f // SQUARES][:, square : square + P], column, plus[:])
 
-        def spread_all(dest, combo):
-            for bank, cols in enumerate(banks):
-                total = (flips, diff_sums)[bank].tile([P, BANK], F32, name="total")
-                spread(total, combo, bank, alone=True)
-                nc.scalar.copy(dest[:, cols], total[:])
+        def spread_thr(bank):
+            for square in range(SQUARES):
+                f = bank * SQUARES + square
+                column = thr_column[:, f : f + 1].to_broadcast([P, P])
+                nc.tensor.transpose(thr_banks[bank][:, square * P : (square + 1) * P], column, plus[:])
 
         step_all = held.tile([P, COMBOS * H], F32, name="step_all")
+
+        def spread_step(j, bank):
+            total = (flips, diff_sums)[bank].tile([P, BANK], F32, name="total")
+            spread(total, STEP + j, bank, alone=True)
+            first = j * H + bank * BANK
+            nc.scalar.copy(step_all[:, first : first + BANK], total[:])
+
+        for bank in range(len(x_banks)):
+            spread_thr(bank)
         for j in (3, 2, 1, 0):
-            spread_all(step_all[:, j * H : (j + 1) * H], STEP + j)
+            for bank in range(len(banks)):
+                spread_step(j, bank)
 
         def picked(bits, entry, count):
             return bits[:].indirect(offsets[:, entry // 16 : (entry + count) // 16])
@@ -116,54 +117,74 @@ def tile_dwnmodel_kernel(tc, x, thr, luts, offs, out):
             count = dest.shape[1]
             nc.vector.tensor_tensor(dest, picked(bits, entry, count), factor, ALU.mult)
 
-        def product(block, p, j):
-            picked_product(p[:], all_bits[block], 0, step_all[:, j * H : (j + 1) * H])
+        def product(block, p, j, width=H):
+            for first in range(0, H, width):
+                factor = step_all[:, j * H + first : j * H + first + width]
+                picked_product(p[:, first : first + width], all_bits[block], first, factor)
 
-        def flip_squares(source, bank):
-            flip = flips.tile([P, BANK], F32, name="total")
+        def add_flipped(total, source, bank, start=False, stop=False):
             for square in range(SQUARES):
                 a = bank * SQUARES + square
-                nc.tensor.transpose(flip[:, square * P : (square + 1) * P], source[:, a * P : (a + 1) * P], plus[:])
-            return flip
+                nc.tensor.matmul(
+                    total[:, square * P : (square + 1) * P],
+                    source[:, a * P : (a + 1) * P],
+                    plus[:],
+                    start=start and square == 0,
+                    stop=stop and square == SQUARES - 1,
+                    is_transpose=True,
+                )
+
+        def flip_back(dest, totals, j):
+            flipped = work.tile([P, H], F32, name="flipped")
+            for a in range(ROWS):
+                part = totals[a // SQUARES][:, (a % SQUARES) * P : (a % SQUARES + 1) * P]
+                bias = combos[:, LOW + j, a : a + 1]
+                nc.scalar.activation(flipped[:, a * P : (a + 1) * P], part, ACT.Identity, bias=bias)
+            for bank, cols in enumerate(banks):
+                flip = flips.tile([P, BANK], F32, name="total")
+                add_flipped(flip, flipped, bank, start=True, stop=True)
+                nc.scalar.copy(dest[:, cols], flip[:])
 
         def first_sums(block):
             upper = work.tile([P, 2 * H], F32, name="upper")
             for e in (1, 0):
                 p = products.tile([P, H], F32, name="product")
-                product(block, p, 2 + e)
-                flipped = work.tile([P, H], F32, name="flipped", bufs=2)
+                product(block, p, 2 + e, width=BANK if block == 0 and e == 1 else H)
+                totals = [flips.tile([P, BANK], F32, name="total") for cols in banks]
                 for bank in range(len(banks)):
-                    flip = flip_squares(p, bank)
-                    for square in range(SQUARES):
-                        a = bank * SQUARES + square
-                        bias = combos[:, LOW + 2 + e, a : a + 1]
-                        part = flip[:, square * P : (square + 1) * P]
-                        nc.scalar.activation(flipped[:, a * P : (a + 1) * P], part, ACT.Identity, bias=bias)
-                for bank, cols in enumerate(banks):
-                    flip = flip_squares(flipped, bank)
-                    nc.scalar.copy(upper[:, e * H + cols.start : e * H + cols.stop], flip[:])
+                    add_flipped(totals[bank], p, bank, start=True, stop=True)
+                flip_back(upper[:, e * H : (e + 1) * H], totals, 2 + e)
             return upper
 
-        def sum_of_two(block, e, upper, sums, stop):
-            p = products.tile([P, H], F32, name="product")
-            product(block, p, e)
-            total = [sums.tile([P, BANK], F32, name="total") for bank in banks]
-            accumulate(total, p, start=True)
-            for bank in range(len(banks)):
-                spread(total[bank], LOW + e, bank)
-            q = products.tile([P, H], F32, name="product")
-            picked_product(q[:], all_bits[block], H, upper[:, e * H : (e + 1) * H])
-            accumulate(total, q, stop=stop)
-            return total
-
         def sum_b_diff(block, upper):
-            b_diff_sum = sum_of_two(block, 1, upper, diff_sums, stop=True)
+            p = products.tile([P, H], F32, name="product")
+            product(block, p, 1)
+            totals = [diff_sums.tile([P, BANK], F32, name="total") for cols in banks]
+            for bank in range(len(banks)):
+                add_flipped(totals[bank], p, bank, start=True)
+            q = products.tile([P, H], F32, name="product")
+            picked_product(q[:], all_bits[block], H, upper[:, H : 2 * H])
+            for bank in range(len(banks)):
+                add_flipped(totals[bank], q, bank, stop=True)
             b_diff = work.tile([P, H], F32, name="b_diff")
-            copy_out(b_diff, b_diff_sum)
+            flip_back(b_diff, totals, 1)
             return b_diff
 
         def sum_out(block, upper):
-            return sum_of_two(block, 0, upper, out_sums, stop=block == blocks - 1)
+            last = block == blocks - 1
+            p = products.tile([P, H], F32, name="product")
+            product(block, p, 0)
+            total = [out_sums.tile([P, BANK], F32, name="total") for cols in banks]
+            accumulate(total, p, start=True)
+            for bank in range(len(banks)):
+                spread(total[bank], LOW, bank)
+            q = products.tile([P, H], F32, name="product")
+            width = BANK if last else H
+            for first in range(0, H, width):
+                part = slice(first, first + width)
+                picked_product(q[:, part], all_bits[block], H + first, upper[:, part])
+            accumulate(total, q, stop=last)
+            return total
 
         def second_sums(block, upper):
             return sum_b_diff(block, upper), sum_out(block, upper)
@@ -193,14 +214,14 @@ def tile_dwnmodel_kernel(tc, x, thr, luts, offs, out):
                 nc.vector.tensor_tensor(bits[:, cols], x_blocks[block][:, cols], thr_bank[:], ALU.is_gt)
             all_bits[block] = bits
 
-        def signs_of(pair):
-            signs = work.tile([P, FLIPS, len(pair) * P], BF16, name="signs", bufs=1)
-            width = len(pair) * P
+        def signs_of(some):
+            width = len(some) * P
+            signs = held.tile([P, FLIPS, width], BF16, name="signs")
             for first in range(0, FLIPS, BANK // width):
                 total = diff_sums.tile([P, BANK], F32, name="total")
                 for k in range(BANK // width):
                     f = first + k
-                    for i, block in enumerate(pair):
+                    for i, block in enumerate(some):
                         square = x_blocks[block][:, f * P : (f + 1) * P]
                         nc.tensor.transpose(total[:, k * width + i * P : k * width + (i + 1) * P], square, plus[:])
                     bias = thr_column[:, f : f + 1]

@@ -24,7 +24,7 @@ HIGH = COMBOS
 STEP = 2 * COMBOS
 MIXES = 3 * COMBOS
 
-RING = 4
+RING = 6
 
 WORK_SETS = 3
 
@@ -189,9 +189,9 @@ def tile_dwnmodel_kernel(tc, x, thr, luts, offs, out):
         def second_sums(block, upper):
             return sum_b_diff(block, upper), sum_out(block, upper)
 
-        def products_s(block, b_diff):
+        def products_s(block, b_diff, pieces):
             s = products.tile([P, H], F32, name="product")
-            for cols in banks:
+            for cols in pieces:
                 picked_product(s[:, cols], all_bits[block], 2 * H + cols.start, b_diff[:, cols])
             return s
 
@@ -199,7 +199,7 @@ def tile_dwnmodel_kernel(tc, x, thr, luts, offs, out):
             nc.sync.dma_start(out[block * P : (block + 1) * P, cols], result[:, cols])
 
         def third_fold(block, b_diff, out_sum):
-            s = products_s(block, b_diff)
+            s = products_s(block, b_diff, banks)
             accumulate(out_sum, s, stop=True)
             result = work.tile([P, H], F32, name="result", bufs=2)
             for bank, cols in zip(out_sum, banks):
@@ -256,8 +256,11 @@ def tile_dwnmodel_kernel(tc, x, thr, luts, offs, out):
         b_diff = sum_b_diff(3, upper[3])
         third_fold(2, *ready[2])
         out_sum = sum_out(3, upper[3])
-        s = products_s(3, b_diff)
+        pieces = [slice(0, BANK), slice(BANK, BANK + BANK // 2), slice(BANK + BANK // 2, H)]
+        s = products_s(3, b_diff, pieces)
         result = work.tile([P, H], F32, name="result", bufs=2)
-        for bank, cols in zip(out_sum, banks):
-            nc.vector.tensor_add(result[:, cols], bank[:], s[:, cols])
+        for cols in pieces:
+            bank, first = divmod(cols.start, BANK)
+            part = out_sum[bank][:, first : first + cols.stop - cols.start]
+            nc.vector.tensor_add(result[:, cols], part, s[:, cols])
             store(3, result, cols)

import concourse.mybir as mybir
from concourse.masks import make_identity

F32 = mybir.dt.float32
BF16 = mybir.dt.bfloat16
U16 = mybir.dt.uint16
ALU = mybir.AluOpType
ACT = mybir.ActivationFunctionType

P = 128
C = 512
S = 2048
H = 1024
E = 8
FOLDS = 3
FLIPS = S // P
COMBOS = E // 2
ROWS = H // P
BANK = 512
SQUARES = BANK // P

LOW = 0
HIGH = COMBOS
STEP = 2 * COMBOS
MIXES = 3 * COMBOS

RING = 6

WORK_SETS = 3


def tile_dwnmodel_kernel(tc, x, thr, luts, offs, out):
    nc = tc.nc
    with (
        tc.tile_pool(name="held", bufs=1) as held,
        tc.tile_pool(name="work", bufs=WORK_SETS) as work,
        tc.tile_pool(name="products", bufs=RING) as products,
        tc.psum_pool(name="flips", bufs=2) as flips,
        tc.psum_pool(name="diff_sums", bufs=2) as diff_sums,
        tc.psum_pool(name="out_sums", bufs=4) as out_sums,
    ):
        by_row = held.tile([P, P], F32, name="by_row")
        entries = E * ROWS
        nc.gpsimd.memset(by_row[entries:P, :], 0.0)
        nc.sync.dma_start(by_row[0:entries, :], luts.rearrange("e (a p) -> (e a) p", p=P))
        nc.sync.dma_start(by_row[entries : entries + FLIPS, :], thr.rearrange("one (f p) -> (one f) p", p=P))

        x_blocks = [work.tile([P, S], F32, name="x_block", bufs=4) for block in range(C // P)]
        x_banks = [slice(first, first + BANK) for first in range(0, S, BANK)]
        for cols in x_banks:
            nc.sync.dma_start(x_blocks[0][:, cols], x[0:P, cols])
        offsets = held.tile([P, FOLDS * H // 16], U16, name="offsets")
        nc.sync.dma_start(offsets[:], offs)
        for block in range(1, C // P):
            nc.sync.dma_start(x_blocks[block][:], x[block * P : (block + 1) * P, :])

        plus = held.tile([P, P], F32, name="plus")
        make_identity(nc, plus[:])
        plus_bf16 = held.tile([P, P], BF16, name="plus_bf16")
        nc.gpsimd.tensor_copy(plus_bf16[:], plus[:])

        banks = [slice(bank * BANK, (bank + 1) * BANK) for bank in range(H // BANK)]

        def accumulate(total, term, start=False, stop=False):
            for bank, cols in zip(total, banks):
                nc.tensor.matmul(bank[:], plus[:], term[:, cols], start=start, stop=stop)

        combos = held.tile([P, MIXES, ROWS], F32, name="combos")
        flip = flips.tile([P, BANK], F32, name="total")
        nc.tensor.transpose(flip[:, 0:P], by_row[:], plus[:])
        thr_column = held.tile([P, FLIPS], F32, name="thr_column")
        nc.scalar.copy(thr_column[:], flip[:, entries : entries + FLIPS])
        nc.scalar.copy(combos[:, 0:E, :], flip[:, 0:entries].rearrange("p (e a) -> p e a", e=E))
        ones = combos[:, 0:E, :].rearrange("p (rest one) a -> p rest one a", one=2)
        nc.vector.tensor_sub(ones[:, :, 1:2, :], ones[:, :, 1:2, :], ones[:, :, 0:1, :])
        twos = combos[:, 0:E, :].rearrange("p (rest two one) a -> p rest two (one a)", two=2, one=2)
        nc.vector.tensor_sub(twos[:, :, 1:2, :], twos[:, :, 1:2, :], twos[:, :, 0:1, :])
        nc.vector.tensor_sub(
            combos[:, STEP : STEP + COMBOS, :], combos[:, HIGH : HIGH + COMBOS, :], combos[:, LOW : LOW + COMBOS, :]
        )

        def spread(total, combo, bank, alone=False):
            for square in range(SQUARES):
                a = bank * SQUARES + square
                column = combos[:, combo, a : a + 1].to_broadcast([P, P])
                cols = slice(square * P, (square + 1) * P)
                nc.tensor.matmul(total[:, cols], column, plus[:], start=alone, stop=alone, is_transpose=True)

        thr_banks = [out_sums.tile([P, BANK], F32, name="total") for cols in x_banks]

        def spread_thr(bank):
            for square in range(SQUARES):
                f = bank * SQUARES + square
                column = thr_column[:, f : f + 1].to_broadcast([P, P])
                nc.tensor.transpose(thr_banks[bank][:, square * P : (square + 1) * P], column, plus[:])

        step_all = held.tile([P, COMBOS * H], F32, name="step_all")

        def spread_step(j, bank):
            total = (flips, diff_sums)[bank].tile([P, BANK], F32, name="total")
            spread(total, STEP + j, bank, alone=True)
            first = j * H + bank * BANK
            nc.scalar.copy(step_all[:, first : first + BANK], total[:])

        for bank in range(len(x_banks)):
            spread_thr(bank)
        for j in (3, 2, 1, 0):
            for bank in range(len(banks)):
                spread_step(j, bank)

        def picked(bits, entry, count):
            return bits[:].indirect(offsets[:, entry // 16 : (entry + count) // 16])

        blocks = C // P

        def picked_product(dest, bits, entry, factor):
            count = dest.shape[1]
            nc.vector.tensor_tensor(dest, picked(bits, entry, count), factor, ALU.mult)

        def product(block, p, j, width=H):
            for first in range(0, H, width):
                factor = step_all[:, j * H + first : j * H + first + width]
                picked_product(p[:, first : first + width], all_bits[block], first, factor)

        def add_flipped(total, source, bank, start=False, stop=False):
            for square in range(SQUARES):
                a = bank * SQUARES + square
                nc.tensor.matmul(
                    total[:, square * P : (square + 1) * P],
                    source[:, a * P : (a + 1) * P],
                    plus[:],
                    start=start and square == 0,
                    stop=stop and square == SQUARES - 1,
                    is_transpose=True,
                )

        def flip_back(dest, totals, j):
            flipped = work.tile([P, H], F32, name="flipped")
            for a in range(ROWS):
                part = totals[a // SQUARES][:, (a % SQUARES) * P : (a % SQUARES + 1) * P]
                bias = combos[:, LOW + j, a : a + 1]
                nc.scalar.activation(flipped[:, a * P : (a + 1) * P], part, ACT.Identity, bias=bias)
            for bank, cols in enumerate(banks):
                flip = flips.tile([P, BANK], F32, name="total")
                add_flipped(flip, flipped, bank, start=True, stop=True)
                nc.scalar.copy(dest[:, cols], flip[:])

        def first_sums(block):
            upper = work.tile([P, 2 * H], F32, name="upper")
            for e in (1, 0):
                p = products.tile([P, H], F32, name="product")
                product(block, p, 2 + e, width=BANK if block == 0 and e == 1 else H)
                totals = [flips.tile([P, BANK], F32, name="total") for cols in banks]
                for bank in range(len(banks)):
                    add_flipped(totals[bank], p, bank, start=True, stop=True)
                flip_back(upper[:, e * H : (e + 1) * H], totals, 2 + e)
            return upper

        def sum_b_diff(block, upper):
            p = products.tile([P, H], F32, name="product")
            product(block, p, 1)
            totals = [diff_sums.tile([P, BANK], F32, name="total") for cols in banks]
            for bank in range(len(banks)):
                add_flipped(totals[bank], p, bank, start=True)
            q = products.tile([P, H], F32, name="product")
            picked_product(q[:], all_bits[block], H, upper[:, H : 2 * H])
            for bank in range(len(banks)):
                add_flipped(totals[bank], q, bank, stop=True)
            b_diff = work.tile([P, H], F32, name="b_diff")
            flip_back(b_diff, totals, 1)
            return b_diff

        def sum_out(block, upper):
            last = block == blocks - 1
            p = products.tile([P, H], F32, name="product")
            product(block, p, 0)
            total = [out_sums.tile([P, BANK], F32, name="total") for cols in banks]
            accumulate(total, p, start=True)
            for bank in range(len(banks)):
                spread(total[bank], LOW, bank)
            q = products.tile([P, H], F32, name="product")
            width = BANK if last else H
            for first in range(0, H, width):
                part = slice(first, first + width)
                picked_product(q[:, part], all_bits[block], H + first, upper[:, part])
            accumulate(total, q, stop=last)
            return total

        def second_sums(block, upper):
            return sum_b_diff(block, upper), sum_out(block, upper)

        def products_s(block, b_diff, pieces):
            s = products.tile([P, H], F32, name="product")
            for cols in pieces:
                picked_product(s[:, cols], all_bits[block], 2 * H + cols.start, b_diff[:, cols])
            return s

        def store(block, result, cols):
            nc.sync.dma_start(out[block * P : (block + 1) * P, cols], result[:, cols])

        def third_fold(block, b_diff, out_sum):
            s = products_s(block, b_diff, banks)
            accumulate(out_sum, s, stop=True)
            result = work.tile([P, H], F32, name="result", bufs=2)
            for bank, cols in zip(out_sum, banks):
                nc.scalar.copy(result[:, cols], bank[:])
                store(block, result, cols)

        all_bits = {}

        def compare(block):
            bits = work.tile([P, S], F32, name="bits", bufs=4)
            for cols, thr_bank in zip(x_banks, thr_banks):
                nc.vector.tensor_tensor(bits[:, cols], x_blocks[block][:, cols], thr_bank[:], ALU.is_gt)
            all_bits[block] = bits

        def signs_of(some):
            width = len(some) * P
            signs = held.tile([P, FLIPS, width], BF16, name="signs")
            for first in range(0, FLIPS, BANK // width):
                total = diff_sums.tile([P, BANK], F32, name="total")
                for k in range(BANK // width):
                    f = first + k
                    for i, block in enumerate(some):
                        square = x_blocks[block][:, f * P : (f + 1) * P]
                        nc.tensor.transpose(total[:, k * width + i * P : k * width + (i + 1) * P], square, plus[:])
                    bias = thr_column[:, f : f + 1]
                    part = total[:, k * width : (k + 1) * width]
                    nc.scalar.activation(signs[:, f, :], part, ACT.Sign, bias=bias, scale=-1.0)
            return signs

        def bits_of(signs, i, block):
            bits = work.tile([P, S], F32, name="bits", bufs=4)
            for bank in range(S // BANK):
                total = diff_sums.tile([P, BANK], F32, name="total")
                for k in range(BANK // P):
                    square = signs[:, bank * (BANK // P) + k, i * P : (i + 1) * P]
                    nc.tensor.matmul(total[:, k * P : (k + 1) * P], square, plus_bf16[:], start=True, stop=True)
                nc.scalar.activation(bits[:, bank * BANK : (bank + 1) * BANK], total[:], ACT.Relu, scale=-1.0)
            all_bits[block] = bits

        compare(0)
        signs = signs_of((2, 3))
        bits_of(signs, 0, 2)
        upper = {0: first_sums(0)}
        compare(1)
        upper[1] = first_sums(1)
        ready = {0: second_sums(0, upper[0])}
        bits_of(signs, 1, 3)
        upper[2] = first_sums(2)
        third_fold(0, *ready[0])
        ready[1] = second_sums(1, upper[1])
        upper[3] = first_sums(3)
        third_fold(1, *ready[1])
        ready[2] = second_sums(2, upper[2])
        b_diff = sum_b_diff(3, upper[3])
        third_fold(2, *ready[2])
        out_sum = sum_out(3, upper[3])
        pieces = [slice(0, BANK), slice(BANK, BANK + BANK // 2), slice(BANK + BANK // 2, H)]
        s = products_s(3, b_diff, pieces)
        result = work.tile([P, H], F32, name="result", bufs=2)
        for cols in pieces:
            bank, first = divmod(cols.start, BANK)
            part = out_sum[bank][:, first : first + cols.stop - cols.start]
            nc.vector.tensor_add(result[:, cols], part, s[:, cols])
            store(3, result, cols)
